import numpy as np
import ml_dtypes


def mxq(x, axis, fmt="e4m3"):
    dtype, down = {"e4m3": (ml_dtypes.float8_e4m3fn, 7), "e5m2": (ml_dtypes.float8_e5m2, 14)}[fmt]
    v = np.moveaxis(np.asarray(x, np.float32).astype(ml_dtypes.bfloat16).astype(np.float64), axis, -1)
    blocks = v.reshape(v.shape[:-1] + (-1, 32))
    amax = np.abs(blocks).max(-1, keepdims=True)
    byte = np.maximum(np.where(amax > 0, np.frexp(amax)[1] - 1 + 127, 0) - down, 1)
    scale = np.exp2(byte - 127.0)
    codes = (blocks / scale).astype(np.float32).astype(dtype).astype(np.float64)
    return np.moveaxis((codes * scale).reshape(v.shape), -1, axis)


WIDE = False


def mx_kscale(k):
    if not WIDE:
        return np.ones(k)
    levels = np.array([10, -10, 5, -5, 0])
    a = np.random.permutation(np.resize(levels, k // 512 * 4)).reshape(k // 512, 4)
    idx = np.arange(k)
    return np.exp2(a[idx // 512, idx % 128 // 32])


BF16 = ml_dtypes.bfloat16


def bf(x):
    return np.asarray(x, np.float32).astype(BF16)


def f64(x):
    return np.asarray(x).astype(np.float64)


B, IN, M, OUT = 1024, 1024, 512, 512
F = 2 * M
EPS = 1e-12


def setup_inputs():
    s, t = mx_kscale(IN), mx_kscale(F)
    return {"x": bf(np.random.standard_normal((B, IN)) * s),
            "W1": bf(np.random.standard_normal((IN, F)) / np.sqrt(IN) / s[:, None] * t),
            "b1": bf(np.random.standard_normal(F) * 0.1 * t),
            "W2": bf(np.random.standard_normal((F, M)) / np.sqrt(F) / t[:, None]),
            "b2": bf(np.random.standard_normal(M) * 0.3)}


def reference(x, W1, b1, W2, b2):
    h = np.maximum((mxq(f64(x), 1, "e4m3") @ mxq(f64(W1), 0, "e4m3")) + f64(b1), 0.0)
    v = (mxq(h, 1, "e4m3") @ mxq(f64(W2), 0, "e4m3")) + f64(b2)
    norm = np.sqrt(np.sum(v * v, axis=-1, keepdims=True))
    return v / np.maximum(norm, EPS)

@@ -1,0 +1,231 @@
+from contextlib import ExitStack
+
+import concourse.mybir as mybir
+from concourse.masks import make_identity
+
+F32 = mybir.dt.float32
+BF16 = mybir.dt.bfloat16
+U32 = mybir.dt.uint32
+U8 = mybir.dt.uint8
+FP8X4 = mybir.dt.float8_e4m3fn_x4
+ACT = mybir.ActivationFunctionType
+ALU = mybir.AluOpType
+
+P = 128
+B, IN, F, M = 1024, 1024, 1024, 512
+FLOPS = 2 * B * IN * F + 2 * B * F * M
+EPS = 1e-12
+
+W1_VEC_COLS = 256
+W2_VEC_COLS = 512
+
+
+def tile_geometricmanifoldnetwork_pa_kernel(tc, x, W1, b1, W2, b2, out):
+    nc = tc.nc
+    with ExitStack() as ctx:
+        const = ctx.enter_context(tc.tile_pool(name="const", bufs=1))
+        ld = ctx.enter_context(tc.tile_pool(name="ld", bufs=1))
+        keep = ctx.enter_context(tc.tile_pool(name="keep", bufs=1))
+        grp = ctx.enter_context(tc.tile_pool(name="grp", bufs=4))
+        hpool = ctx.enter_context(tc.tile_pool(name="hpool", bufs=3))
+        work = ctx.enter_context(tc.tile_pool(name="work", bufs=4))
+        psum = ctx.enter_context(tc.psum_pool(name="psum", bufs=8))
+
+        small = const.tile([P, 640], BF16, name="small")
+        nc.vector.memset(small[:], 0.0)
+        nc.scalar.dma_start(out=small[0:8, 512:640], in_=b1.rearrange("(r c) -> r c", c=P))
+        nc.scalar.dma_start(out=small[0:1, 0:512], in_=b2.rearrange("(o m) -> o m", o=1))
+
+        raw1 = [ld.tile([P, 4 * F], BF16, name="raw1_%d" % g) for g in range(2)]
+        for g in range(2):
+            for u in range(2):
+                r0 = 512 * g + 256 * u
+                nc.sync.dma_start(
+                    out=raw1[g][:, 2 * u * F : (2 * u + 2) * F].rearrange("q (e f) -> q e f", e=2),
+                    in_=W1[r0 : r0 + 256, :].rearrange("(q e) f -> q e f", e=2),
+                )
+        xh = [ld.tile([P, 4 * IN], BF16, name="xh_%d" % h) for h in range(2)]
+        x_v = x.rearrange("(p t) k -> p t k", t=8)
+        raw2 = ld.tile([P, 8 * M], BF16, name="raw2")
+        w2_v = W2.rearrange("(j p) m -> p j m", p=P)
+
+        def load_x(h):
+            nc.sync.dma_start(
+                out=xh[h][:].rearrange("p (t k) -> p t k", t=4), in_=x_v[:, 4 * h : 4 * h + 4, :]
+            )
+
+        def load_w2(g):
+            nc.sync.dma_start(
+                out=raw2[:, 4 * g * M : (4 * g + 4) * M].rearrange("p (j m) -> p j m", j=4),
+                in_=w2_v[:, 4 * g : 4 * g + 4, :],
+            )
+
+        load_x(0)
+        load_w2(0)
+        load_w2(1)
+        load_x(1)
+
+        ident_f = const.tile([P, P], F32, name="ident_f")
+        make_identity(nc, ident_f[:])
+        ident_b = const.tile([P, P], BF16, name="ident_b")
+        nc.vector.tensor_copy(out=ident_b[:], in_=ident_f[:])
+        ones_b = const.tile([P, P], BF16, name="ones_b")
+        nc.vector.memset(ones_b[:], 1.0)
+        warm_in = const.tile([P, 1], F32, name="warm_in")
+        warm_out = const.tile([P, 1], F32, name="warm_out")
+        nc.vector.memset(warm_in[:], 1.0)
+        nc.scalar.activation(out=warm_out[:], in_=warm_in[:], func=ACT.Sqrt)
+
+        ps_b2 = psum.tile([P, 512], F32, name="ps_b2", tag="bank")
+        nc.tensor.matmul(out=ps_b2[:], lhsT=ones_b[:], rhs=small[:, 0:512], start=True, stop=True)
+        b2bc = const.tile([P, M], F32, name="b2bc")
+        nc.vector.tensor_copy(out=b2bc[:], in_=ps_b2[:])
+        ps_b1 = psum.tile([P, P], BF16, name="ps_b1", tag="bank")
+        nc.tensor.transpose(out=ps_b1[:], in_=small[:, 512:640], identity=ident_b[:])
+        b1f = const.tile([P, 8], F32, name="b1f")
+        nc.vector.tensor_copy(out=b1f[:], in_=ps_b1[:, 0:8])
+
+        c1 = keep.tile([P, 2, F], U32, name="c1", align_bytes=64)
+        s1 = keep.tile([P, 2, F], U8, name="s1", align_bytes=64)
+        cx = keep.tile([P, 2, B], U32, name="cx", align_bytes=64)
+        sx = keep.tile([P, 2, B], U8, name="sx", align_bytes=64)
+        ch = keep.tile([P, 2, B], U32, name="ch", align_bytes=64)
+        sh = keep.tile([P, 2, B], U8, name="sh", align_bytes=64)
+        c2 = keep.tile([P, 2, M], U32, name="c2", align_bytes=64)
+        s2 = keep.tile([P, 2, M], U8, name="s2", align_bytes=64)
+
+        def regroup(dst, src, vec_cols):
+            d = dst[:].rearrange("p (w t) -> p w t", t=4)
+            if vec_cols > 0:
+                nc.vector.tensor_copy(
+                    out=d[:, 0:vec_cols, :].rearrange("p (c i) t -> p c t i", i=4),
+                    in_=src[:, :, 0:vec_cols].rearrange("p t (c i) -> p c t i", i=4),
+                )
+            if vec_cols < 512:
+                nc.scalar.copy(
+                    out=d[:, vec_cols:512, :].rearrange("p (c i) t -> p c t i", i=4),
+                    in_=src[:, :, vec_cols:512].rearrange("p t (c i) -> p c t i", i=4),
+                )
+
+        def quantise(codes, scales, src):
+            nc.vector.quantize_mx(out=codes.bitcast(FP8X4), scales=scales, in_=src[:])
+
+        def w1_unit(g, fh):
+            gw = grp.tile([P, 2048], BF16, name="gw", tag="grp", align_bytes=64)
+            src = raw1[g][:].rearrange("q (t f) -> q t f", t=4)[:, :, 512 * fh : 512 * fh + 512]
+            regroup(gw, src, W1_VEC_COLS)
+            cols = slice(512 * fh, 512 * fh + 512)
+            quantise(c1[:, g, cols], s1[:, g, cols], gw)
+
+        def w2_unit(g):
+            gw = grp.tile([P, 2048], BF16, name="gw2", tag="grp", align_bytes=64)
+            src = raw2[:, 4 * g * M : (4 * g + 4) * M].rearrange("p (t m) -> p t m", t=4)
+            regroup(gw, src, W2_VEC_COLS)
+            quantise(c2[:, g, :], s2[:, g, :], gw)
+
+        def x_unit(g, bh, engines):
+            gx = grp.tile([P, 2048], BF16, name="gx", tag="grp", align_bytes=64)
+            gx_w = gx[:].bitcast(F32).rearrange("q (a b u) -> q a b u", a=2, u=2)
+            x_w = xh[bh][:].bitcast(F32)
+            for a in range(2):
+                xt = psum.tile([P, 512], F32, name="xt", tag="bank")
+                xt_v = xt[:].rearrange("q (t u b) -> q t u b", t=2, u=2)
+                for t in range(2):
+                    for u in range(2):
+                        c0 = 512 * (2 * a + t) + 256 * g + 128 * u
+                        nc.tensor.transpose(
+                            out=xt_v[:, t, u, :], in_=x_w[:, c0 : c0 + 128], identity=ident_f[:]
+                        )
+                dst = gx_w[:, a, :, :].rearrange("q (t b) u -> q t b u", t=2)
+                src = xt_v.rearrange("q t u b -> q t b u")
+                if engines[a] == "v":
+                    nc.vector.tensor_copy(out=dst, in_=src)
+                else:
+                    nc.scalar.copy(out=dst, in_=src)
+            cols = slice(512 * bh, 512 * bh + 512)
+            quantise(cx[:, g, cols], sx[:, g, cols], gx)
+
+        hts = {}
+
+        def mm1(ft, bh):
+            g2, t = divmod(ft, 4)
+            if t == 0:
+                hts[(g2, bh)] = hpool.tile([P, 4, 512], BF16, name="ht", tag="ht")
+            ph = psum.tile([P, 512], F32, name="ph", tag="bank")
+            fc = slice(P * ft, P * ft + P)
+            bc = slice(512 * bh, 512 * bh + 512)
+            for g in range(2):
+                nc.tensor.matmul_mx(
+                    out=ph[:],
+                    lhsT=c1[:, g, fc].bitcast(FP8X4),
+                    lhsT_scale=s1[:, g, fc],
+                    rhs=cx[:, g, bc].bitcast(FP8X4),
+                    rhs_scale=sx[:, g, bc],
+                    start=(g == 0),
+                    stop=(g == 1),
+                )
+            nc.scalar.activation(
+                out=hts[(g2, bh)][:, t, :], in_=ph[:], func=ACT.Relu, bias=b1f[:, ft : ft + 1], scale=1.0
+            )
+
+        def h_unit(g2, bh):
+            gh = grp.tile([P, 2048], BF16, name="gh", tag="grp", align_bytes=64)
+            regroup(gh, hts[(g2, bh)][:], 512)
+            cols = slice(512 * bh, 512 * bh + 512)
+            quantise(ch[:, g2, cols], sh[:, g2, cols], gh)
+
+        out_v = out.rearrange("(p t) m -> p t m", t=8)
+
+        def mm2(bt):
+            pv = psum.tile([P, 512], F32, name="pv", tag="bank")
+            bc = slice(P * bt, P * bt + P)
+            for g in range(2):
+                nc.tensor.matmul_mx(
+                    out=pv[:],
+                    lhsT=ch[:, g, bc].bitcast(FP8X4),
+                    lhsT_scale=sh[:, g, bc],
+                    rhs=c2[:, g, :].bitcast(FP8X4),
+                    rhs_scale=s2[:, g, :],
+                    start=(g == 0),
+                    stop=(g == 1),
+                )
+            v = work.tile([P, M], F32, name="v", tag="v")
+            nc.vector.tensor_tensor(out=v[:], in0=pv[:], in1=b2bc[:], op=ALU.add)
+            junk = work.tile([P, M], F32, name="junk", tag="junk")
+            ss = work.tile([P, 1], F32, name="ss", tag="ss")
+            ssm = work.tile([P, 1], F32, name="ssm", tag="ssm")
+            nrm = work.tile([P, 1], F32, name="nrm", tag="nrm")
+            rinv = work.tile([P, 1], F32, name="rinv", tag="rinv")
+            nc.scalar.activation(out=junk[:], in_=v[:], func=ACT.Square, accum_out=ss[:])
+            nc.vector.tensor_scalar_max(out=ssm[:], in0=ss[:], scalar1=EPS * EPS)
+            nc.scalar.activation(out=nrm[:], in_=ssm[:], func=ACT.Sqrt)
+            nc.vector.reciprocal(out=rinv[:], in_=nrm[:])
+            o = work.tile([P, M], F32, name="o", tag="o")
+            nc.vector.tensor_scalar_mul(out=o[:], in0=v[:], scalar1=rinv[:])
+            nc.sync.dma_start(out=out_v[:, bt, :], in_=o[:])
+
+        for g in range(2):
+            for fh in range(2):
+                w1_unit(g, fh)
+        x_unit(0, 0, "sv")
+        x_unit(1, 0, "sv")
+        for ft in range(4):
+            mm1(ft, 0)
+        w2_unit(0)
+        h_unit(0, 0)
+        for ft in range(4, 8):
+            mm1(ft, 0)
+        w2_unit(1)
+        x_unit(0, 1, "ss")
+        x_unit(1, 1, "ss")
+        h_unit(1, 0)
+        for bt in range(4):
+            mm2(bt)
+        for ft in range(4):
+            mm1(ft, 1)
+        h_unit(0, 1)
+        for ft in range(4, 8):
+            mm1(ft, 1)
+        h_unit(1, 1)
+        for bt in range(4, 8):
+            mm2(bt)

@@ -16,216 +16,375 @@ B, IN, F, M = 1024, 1024, 1024, 512
 FLOPS = 2 * B * IN * F + 2 * B * F * M
 EPS = 1e-12
 
-W1_VEC_COLS = 256
-W2_VEC_COLS = 512
+PROGRAM = [
+    ("ld_w1r", 1, 0),
+    ("ld_small",),
+    ("ld_w1r", 1, 1),
+    ("sb2m",),
+    ("ld_x", 0),
+    ("ld_x", 1),
+    ("sb2c", "S"),
+    ("w1r", 1, 0, "V", 256, 512),
+    ("xt", 0, 0, 0),
+    ("xt", 0, 0, 1),
+    ("w1r", 1, 1, "S", 256, 512),
+    ("xe", 0, 0, 0, "S"),
+    ("ld_w1r", 0, 0),
+    ("w1r", 1, 1, "V", 0, 256),
+    ("ld_w1r", 0, 1),
+    ("xt", 1, 0, 1),
+    ("ld_x", 2),
+    ("xe", 0, 0, 1, "S"),
+    ("xe", 1, 0, 1, "S"),
+    ("xt", 1, 0, 0),
+    ("ld_x", 3),
+    ("w1q", 1, 1),
+    ("ld_w2", 0),
+    ("w1r", 1, 0, "V", 0, 256),
+    ("w1q", 1, 0),
+    ("xq", 0, 0),
+    ("sb1t",),
+    ("xe", 1, 0, 0, "S"),
+    ("w1r", 0, 0, "S", 256, 512),
+    ("xt", 1, 1, 0),
+    ("xq", 1, 0),
+    ("ld_w2", 1),
+    ("w1r", 0, 1, "S", 256, 512),
+    ("xe", 1, 1, 0, "S"),
+    ("w1r", 0, 0, "V", 0, 256),
+    ("sb1c", "V"),
+    ("xt", 1, 1, 1),
+    ("w1q", 0, 0),
+    ("m1", 1, 0),
+    ("m1", 3, 0),
+    ("m1", 0, 0),
+    ("xt", 0, 1, 1),
+    ("w1r", 0, 1, "V", 0, 256),
+    ("w1q", 0, 1),
+    ("xe", 1, 1, 1, "S"),
+    ("xq", 1, 1),
+    ("w2r", 0, "V", 256, 512),
+    ("he", 1, 0, "S"),
+    ("xt", 0, 1, 0),
+    ("he", 3, 0, "S"),
+    ("m1", 6, 0),
+    ("he", 0, 0, "V"),
+    ("m1", 7, 0),
+    ("xe", 0, 1, 0, "V"),
+    ("xe", 0, 1, 1, "S"),
+    ("m1", 4, 0),
+    ("w2r", 1, "S", 256, 512),
+    ("w2r", 1, "V", 0, 256),
+    ("m1", 5, 0),
+    ("he", 6, 0, "S"),
+    ("xq", 0, 1),
+    ("m1", 2, 0),
+    ("he", 4, 0, "S"),
+    ("w2q", 1),
+    ("he", 7, 0, "V"),
+    ("m1", 6, 1),
+    ("w2r", 0, "V", 0, 256),
+    ("m1", 4, 1),
+    ("he", 5, 0, "S"),
+    ("hr", 1, 0, "V", 0, 256),
+    ("he", 2, 0, "S"),
+    ("w2q", 0),
+    ("he", 6, 1, "S"),
+    ("he", 4, 1, "S"),
+    ("hr", 0, 0, "V", 0, 256),
+    ("m1", 3, 1),
+    ("m1", 0, 1),
+    ("hr", 0, 0, "V", 256, 512),
+    ("m1", 5, 1),
+    ("he", 3, 1, "S"),
+    ("m1", 7, 1),
+    ("m1", 1, 1),
+    ("hr", 1, 0, "S", 256, 512),
+    ("he", 7, 1, "S"),
+    ("he", 1, 1, "S"),
+    ("he", 0, 1, "V"),
+    ("he", 5, 1, "V"),
+    ("hq", 1, 0),
+    ("m1", 2, 1),
+    ("he", 2, 1, "S"),
+    ("hq", 0, 0),
+    ("hr", 1, 1, "S", 0, 256),
+    ("hr", 1, 1, "V", 256, 512),
+    ("m2", 2),
+    ("hr", 0, 1, "V", 0, 256),
+    ("va", 2),
+    ("hr", 0, 1, "S", 256, 512),
+    ("sq", 2, 0, 2),
+    ("m2", 1),
+    ("va", 1),
+    ("hq", 1, 1),
+    ("m2", 0),
+    ("hq", 0, 1),
+    ("m2", 3),
+    ("va", 0),
+    ("va", 3),
+    ("sq", 1, 0, 1),
+    ("m2", 5),
+    ("sq", 0, 0, 0),
+    ("va", 5),
+    ("sq", 3, 0, 3),
+    ("tmax", 0, 4),
+    ("m2", 4),
+    ("sq", 5, 1, 1),
+    ("va", 4),
+    ("tsqrt", 0, 4),
+    ("m2", 6),
+    ("trec", 0, 4),
+    ("sc", 3, "V", 0, 3, 1, 1, 2),
+    ("m2", 7),
+    ("sc", 2, "V", 0, 2, 1, 0, 2),
+    ("sq", 4, 1, 0),
+    ("tmax", 1, 2),
+    ("va", 6),
+    ("sc", 0, "S", 0, 0, 0, 0, 2),
+    ("sc", 1, "V", 0, 1, 0, 1, 2),
+    ("tsqrt", 1, 2),
+    ("sq", 6, 2, 0),
+    ("trec", 1, 2),
+    ("va", 7),
+    ("sc", 5, "V", 1, 1, 2, 1, 2),
+    ("sc", 4, "V", 1, 0, 2, 0, 2),
+    ("sq", 7, 2, 1),
+    ("st", 1, 2, 2),
+    ("tmax", 2, 2),
+    ("tsqrt", 2, 2),
+    ("st", 0, 0, 2),
+    ("trec", 2, 2),
+    ("sc", 7, "S", 2, 1, 4, 0, 1),
+    ("sc", 6, "V", 2, 0, 3, 0, 1),
+    ("st", 2, 4, 2),
+    ("st", 3, 6, 1),
+    ("st", 4, 7, 1),
+]
 
 
 def tile_geometricmanifoldnetwork_pa_kernel(tc, x, W1, b1, W2, b2, out):
     nc = tc.nc
     with ExitStack() as ctx:
-        const = ctx.enter_context(tc.tile_pool(name="const", bufs=1))
-        ld = ctx.enter_context(tc.tile_pool(name="ld", bufs=1))
-        keep = ctx.enter_context(tc.tile_pool(name="keep", bufs=1))
-        grp = ctx.enter_context(tc.tile_pool(name="grp", bufs=4))
-        hpool = ctx.enter_context(tc.tile_pool(name="hpool", bufs=3))
-        work = ctx.enter_context(tc.tile_pool(name="work", bufs=4))
-        psum = ctx.enter_context(tc.psum_pool(name="psum", bufs=8))
+        sb = ctx.enter_context(tc.tile_pool(name="sb", bufs=1))
+        ps_t = ctx.enter_context(tc.psum_pool(name="ps_t", bufs=2))
+        ps_h = ctx.enter_context(tc.psum_pool(name="ps_h", bufs=4))
+        ps_v = ctx.enter_context(tc.psum_pool(name="ps_v", bufs=2))
+        ctx.enter_context(tc.manual_schedule())
 
-        small = const.tile([P, 640], BF16, name="small")
-        nc.vector.memset(small[:], 0.0)
-        nc.scalar.dma_start(out=small[0:8, 512:640], in_=b1.rearrange("(r c) -> r c", c=P))
-        nc.scalar.dma_start(out=small[0:1, 0:512], in_=b2.rearrange("(o m) -> o m", o=1))
+        tiles = {}
 
-        raw1 = [ld.tile([P, 4 * F], BF16, name="raw1_%d" % g) for g in range(2)]
-        for g in range(2):
-            for u in range(2):
-                r0 = 512 * g + 256 * u
-                nc.sync.dma_start(
-                    out=raw1[g][:, 2 * u * F : (2 * u + 2) * F].rearrange("q (e f) -> q e f", e=2),
-                    in_=W1[r0 : r0 + 256, :].rearrange("(q e) f -> q e f", e=2),
-                )
-        xh = [ld.tile([P, 4 * IN], BF16, name="xh_%d" % h) for h in range(2)]
+        def get(key, shape, dtype):
+            if key not in tiles:
+                tiles[key] = sb.tile(shape, dtype, name=key, align_bytes=64)
+            return tiles[key]
+
         x_v = x.rearrange("(p t) k -> p t k", t=8)
-        raw2 = ld.tile([P, 8 * M], BF16, name="raw2")
         w2_v = W2.rearrange("(j p) m -> p j m", p=P)
-
-        def load_x(h):
-            nc.sync.dma_start(
-                out=xh[h][:].rearrange("p (t k) -> p t k", t=4), in_=x_v[:, 4 * h : 4 * h + 4, :]
-            )
-
-        def load_w2(g):
-            nc.sync.dma_start(
-                out=raw2[:, 4 * g * M : (4 * g + 4) * M].rearrange("p (j m) -> p j m", j=4),
-                in_=w2_v[:, 4 * g : 4 * g + 4, :],
-            )
-
-        load_x(0)
-        load_w2(0)
-        load_w2(1)
-        load_x(1)
-
-        ident_f = const.tile([P, P], F32, name="ident_f")
-        make_identity(nc, ident_f[:])
-        ident_b = const.tile([P, P], BF16, name="ident_b")
-        nc.vector.tensor_copy(out=ident_b[:], in_=ident_f[:])
-        ones_b = const.tile([P, P], BF16, name="ones_b")
-        nc.vector.memset(ones_b[:], 1.0)
-        warm_in = const.tile([P, 1], F32, name="warm_in")
-        warm_out = const.tile([P, 1], F32, name="warm_out")
-        nc.vector.memset(warm_in[:], 1.0)
-        nc.scalar.activation(out=warm_out[:], in_=warm_in[:], func=ACT.Sqrt)
-
-        ps_b2 = psum.tile([P, 512], F32, name="ps_b2", tag="bank")
-        nc.tensor.matmul(out=ps_b2[:], lhsT=ones_b[:], rhs=small[:, 0:512], start=True, stop=True)
-        b2bc = const.tile([P, M], F32, name="b2bc")
-        nc.vector.tensor_copy(out=b2bc[:], in_=ps_b2[:])
-        ps_b1 = psum.tile([P, P], BF16, name="ps_b1", tag="bank")
-        nc.tensor.transpose(out=ps_b1[:], in_=small[:, 512:640], identity=ident_b[:])
-        b1f = const.tile([P, 8], F32, name="b1f")
-        nc.vector.tensor_copy(out=b1f[:], in_=ps_b1[:, 0:8])
-
-        c1 = keep.tile([P, 2, F], U32, name="c1", align_bytes=64)
-        s1 = keep.tile([P, 2, F], U8, name="s1", align_bytes=64)
-        cx = keep.tile([P, 2, B], U32, name="cx", align_bytes=64)
-        sx = keep.tile([P, 2, B], U8, name="sx", align_bytes=64)
-        ch = keep.tile([P, 2, B], U32, name="ch", align_bytes=64)
-        sh = keep.tile([P, 2, B], U8, name="sh", align_bytes=64)
-        c2 = keep.tile([P, 2, M], U32, name="c2", align_bytes=64)
-        s2 = keep.tile([P, 2, M], U8, name="s2", align_bytes=64)
-
-        def regroup(dst, src, vec_cols):
-            d = dst[:].rearrange("p (w t) -> p w t", t=4)
-            if vec_cols > 0:
-                nc.vector.tensor_copy(
-                    out=d[:, 0:vec_cols, :].rearrange("p (c i) t -> p c t i", i=4),
-                    in_=src[:, :, 0:vec_cols].rearrange("p t (c i) -> p c t i", i=4),
-                )
-            if vec_cols < 512:
-                nc.scalar.copy(
-                    out=d[:, vec_cols:512, :].rearrange("p (c i) t -> p c t i", i=4),
-                    in_=src[:, :, vec_cols:512].rearrange("p t (c i) -> p c t i", i=4),
-                )
-
-        def quantise(codes, scales, src):
-            nc.vector.quantize_mx(out=codes.bitcast(FP8X4), scales=scales, in_=src[:])
-
-        def w1_unit(g, fh):
-            gw = grp.tile([P, 2048], BF16, name="gw", tag="grp", align_bytes=64)
-            src = raw1[g][:].rearrange("q (t f) -> q t f", t=4)[:, :, 512 * fh : 512 * fh + 512]
-            regroup(gw, src, W1_VEC_COLS)
-            cols = slice(512 * fh, 512 * fh + 512)
-            quantise(c1[:, g, cols], s1[:, g, cols], gw)
-
-        def w2_unit(g):
-            gw = grp.tile([P, 2048], BF16, name="gw2", tag="grp", align_bytes=64)
-            src = raw2[:, 4 * g * M : (4 * g + 4) * M].rearrange("p (t m) -> p t m", t=4)
-            regroup(gw, src, W2_VEC_COLS)
-            quantise(c2[:, g, :], s2[:, g, :], gw)
-
-        def x_unit(g, bh, engines):
-            gx = grp.tile([P, 2048], BF16, name="gx", tag="grp", align_bytes=64)
-            gx_w = gx[:].bitcast(F32).rearrange("q (a b u) -> q a b u", a=2, u=2)
-            x_w = xh[bh][:].bitcast(F32)
-            for a in range(2):
-                xt = psum.tile([P, 512], F32, name="xt", tag="bank")
-                xt_v = xt[:].rearrange("q (t u b) -> q t u b", t=2, u=2)
-                for t in range(2):
-                    for u in range(2):
-                        c0 = 512 * (2 * a + t) + 256 * g + 128 * u
-                        nc.tensor.transpose(
-                            out=xt_v[:, t, u, :], in_=x_w[:, c0 : c0 + 128], identity=ident_f[:]
-                        )
-                dst = gx_w[:, a, :, :].rearrange("q (t b) u -> q t b u", t=2)
-                src = xt_v.rearrange("q t u b -> q t b u")
-                if engines[a] == "v":
-                    nc.vector.tensor_copy(out=dst, in_=src)
-                else:
-                    nc.scalar.copy(out=dst, in_=src)
-            cols = slice(512 * bh, 512 * bh + 512)
-            quantise(cx[:, g, cols], sx[:, g, cols], gx)
-
-        hts = {}
-
-        def mm1(ft, bh):
-            g2, t = divmod(ft, 4)
-            if t == 0:
-                hts[(g2, bh)] = hpool.tile([P, 4, 512], BF16, name="ht", tag="ht")
-            ph = psum.tile([P, 512], F32, name="ph", tag="bank")
-            fc = slice(P * ft, P * ft + P)
-            bc = slice(512 * bh, 512 * bh + 512)
-            for g in range(2):
-                nc.tensor.matmul_mx(
-                    out=ph[:],
-                    lhsT=c1[:, g, fc].bitcast(FP8X4),
-                    lhsT_scale=s1[:, g, fc],
-                    rhs=cx[:, g, bc].bitcast(FP8X4),
-                    rhs_scale=sx[:, g, bc],
-                    start=(g == 0),
-                    stop=(g == 1),
-                )
-            nc.scalar.activation(
-                out=hts[(g2, bh)][:, t, :], in_=ph[:], func=ACT.Relu, bias=b1f[:, ft : ft + 1], scale=1.0
-            )
-
-        def h_unit(g2, bh):
-            gh = grp.tile([P, 2048], BF16, name="gh", tag="grp", align_bytes=64)
-            regroup(gh, hts[(g2, bh)][:], 512)
-            cols = slice(512 * bh, 512 * bh + 512)
-            quantise(ch[:, g2, cols], sh[:, g2, cols], gh)
-
         out_v = out.rearrange("(p t) m -> p t m", t=8)
 
-        def mm2(bt):
-            pv = psum.tile([P, 512], F32, name="pv", tag="bank")
-            bc = slice(P * bt, P * bt + P)
+        small = get("small", [P, 640], BF16)
+        nc.vector.memset(small[:], 0.0)
+        ones_b = get("ones_b", [P, P], BF16)
+        nc.vector.memset(ones_b[:], 1.0)
+        warm_in = get("warm_in", [P, 1], F32)
+        warm_out = get("warm_out", [P, 1], F32)
+        nc.vector.memset(warm_in[:], 1.0)
+        nc.scalar.activation(out=warm_out[:], in_=warm_in[:], func=ACT.Sqrt)
+        ident_f = get("ident_f", [P, P], F32)
+        make_identity(nc, ident_f[:])
+        ident_b = get("ident_b", [P, P], BF16)
+        nc.vector.tensor_copy(out=ident_b[:], in_=ident_f[:])
+        b1f = get("b1f", [P, 8], F32)
+        b2bc = get("b2bc", [P, M], F32)
+        junk = get("junk", [P, M], F32)
+
+        def copy_on(e, dst, src):
+            if e == "V":
+                nc.vector.tensor_copy(out=dst, in_=src)
+            else:
+                nc.scalar.copy(out=dst, in_=src)
+
+        def regroup(e, dst, src, c0, c1):
+            d = dst[:].rearrange("p (w t) -> p w t", t=4)
+            copy_on(
+                e,
+                d[:, c0:c1, :].rearrange("p (c i) t -> p c t i", i=4),
+                src[:, :, c0:c1].rearrange("p t (c i) -> p c t i", i=4),
+            )
+
+        def quantise(name, src):
+            codes = get("c_" + name, [P, 512], U32)
+            scales = get("s_" + name, [P, 512], U8)
+            nc.vector.quantize_mx(out=codes[:].bitcast(FP8X4), scales=scales[:], in_=src[:])
+
+        def mx_group(acc, lhs_names, lcols, rhs_names):
             for g in range(2):
                 nc.tensor.matmul_mx(
-                    out=pv[:],
-                    lhsT=ch[:, g, bc].bitcast(FP8X4),
-                    lhsT_scale=sh[:, g, bc],
-                    rhs=c2[:, g, :].bitcast(FP8X4),
-                    rhs_scale=s2[:, g, :],
+                    out=acc[:],
+                    lhsT=tiles["c_" + lhs_names[g]][:, lcols].bitcast(FP8X4),
+                    lhsT_scale=tiles["s_" + lhs_names[g]][:, lcols],
+                    rhs=tiles["c_" + rhs_names[g]][:].bitcast(FP8X4),
+                    rhs_scale=tiles["s_" + rhs_names[g]][:],
                     start=(g == 0),
                     stop=(g == 1),
                 )
-            v = work.tile([P, M], F32, name="v", tag="v")
-            nc.vector.tensor_tensor(out=v[:], in0=pv[:], in1=b2bc[:], op=ALU.add)
-            junk = work.tile([P, M], F32, name="junk", tag="junk")
-            ss = work.tile([P, 1], F32, name="ss", tag="ss")
-            ssm = work.tile([P, 1], F32, name="ssm", tag="ssm")
-            nrm = work.tile([P, 1], F32, name="nrm", tag="nrm")
-            rinv = work.tile([P, 1], F32, name="rinv", tag="rinv")
-            nc.scalar.activation(out=junk[:], in_=v[:], func=ACT.Square, accum_out=ss[:])
-            nc.vector.tensor_scalar_max(out=ssm[:], in0=ss[:], scalar1=EPS * EPS)
-            nc.scalar.activation(out=nrm[:], in_=ssm[:], func=ACT.Sqrt)
-            nc.vector.reciprocal(out=rinv[:], in_=nrm[:])
-            o = work.tile([P, M], F32, name="o", tag="o")
-            nc.vector.tensor_scalar_mul(out=o[:], in0=v[:], scalar1=rinv[:])
-            nc.sync.dma_start(out=out_v[:, bt, :], in_=o[:])
 
-        for g in range(2):
-            for fh in range(2):
-                w1_unit(g, fh)
-        x_unit(0, 0, "sv")
-        x_unit(1, 0, "sv")
-        for ft in range(4):
-            mm1(ft, 0)
-        w2_unit(0)
-        h_unit(0, 0)
-        for ft in range(4, 8):
-            mm1(ft, 0)
-        w2_unit(1)
-        x_unit(0, 1, "ss")
-        x_unit(1, 1, "ss")
-        h_unit(1, 0)
-        for bt in range(4):
-            mm2(bt)
-        for ft in range(4):
-            mm1(ft, 1)
-        h_unit(0, 1)
-        for ft in range(4, 8):
-            mm1(ft, 1)
-        h_unit(1, 1)
-        for bt in range(4, 8):
-            mm2(bt)
+        def ld_small():
+            nc.sync.dma_start(out=small[0:8, 512:640], in_=b1.rearrange("(r c) -> r c", c=P))
+            nc.sync.dma_start(out=small[0:1, 0:512], in_=b2.rearrange("(o m) -> o m", o=1))
+
+        def ld_w1r(g, u):
+            raw = get("raw1_%d" % g, [P, 4, F], BF16)
+            r0 = 512 * g + 256 * u
+            nc.sync.dma_start(
+                out=raw[:, 2 * u : 2 * u + 2, :], in_=W1[r0 : r0 + 256, :].rearrange("(q e) f -> q e f", e=2)
+            )
+
+        def ld_w1c(g, fh, u):
+            raw = get("raw1_%d%d" % (g, fh), [P, 4, 512], BF16)
+            r0 = 512 * g + 256 * u
+            nc.sync.dma_start(
+                out=raw[:, 2 * u : 2 * u + 2, :],
+                in_=W1[r0 : r0 + 256, 512 * fh : 512 * fh + 512].rearrange("(q e) f -> q e f", e=2),
+            )
+
+        def ld_x(j):
+            xp = get("x_%d" % j, [P, 2, IN], BF16)
+            nc.sync.dma_start(out=xp[:], in_=x_v[:, 2 * j : 2 * j + 2, :])
+
+        def ld_w2(g):
+            raw = get("raw2_%d" % g, [P, 4, M], BF16)
+            nc.sync.dma_start(out=raw[:], in_=w2_v[:, 4 * g : 4 * g + 4, :])
+
+        def sb1t():
+            pb = ps_t.tile([P, P], BF16, name="pb", tag="t")
+            tiles["pb"] = pb
+            nc.tensor.transpose(out=pb[:], in_=small[:, 512:640], identity=ident_b[:])
+
+        def sb1c(e):
+            copy_on(e, b1f[:], tiles["pb"][:, 0:8])
+
+        def sb2m():
+            pb2 = ps_v.tile([P, M], F32, name="pb2", tag="v")
+            tiles["pb2"] = pb2
+            nc.tensor.matmul(out=pb2[:], lhsT=ones_b[:], rhs=small[:, 0:512], start=True, stop=True)
+
+        def sb2c(e):
+            copy_on(e, b2bc[:], tiles["pb2"][:])
+
+        def w1r(g, fh, e, c0, c1):
+            if ("raw1_%d%d" % (g, fh)) in tiles:
+                src = tiles["raw1_%d%d" % (g, fh)][:]
+            else:
+                src = tiles["raw1_%d" % g][:, :, 512 * fh : 512 * fh + 512]
+            regroup(e, get("g_w1_%d%d" % (g, fh), [P, 2048], BF16), src, c0, c1)
+
+        def w1q(g, fh):
+            quantise("w1_%d%d" % (g, fh), tiles["g_w1_%d%d" % (g, fh)])
+
+        def w2r(g, e, c0, c1):
+            regroup(e, get("g_w2_%d" % g, [P, 2048], BF16), tiles["raw2_%d" % g][:], c0, c1)
+
+        def w2q(g):
+            quantise("w2_%d" % g, tiles["g_w2_%d" % g])
+
+        def xt(g, bh, a):
+            pt = ps_t.tile([P, 2, 2, P], F32, name="pt", tag="t")
+            tiles["pt_%d%d%d" % (g, bh, a)] = pt
+            x_w = tiles["x_%d" % (2 * bh + a)][:].rearrange("p t k -> p (t k)").bitcast(F32)
+            for t in range(2):
+                for u in range(2):
+                    c0 = 512 * t + 256 * g + 128 * u
+                    nc.tensor.transpose(out=pt[:, t, u, :], in_=x_w[:, c0 : c0 + 128], identity=ident_f[:])
+
+        def xe(g, bh, a, e):
+            gx = get("g_x_%d%d" % (g, bh), [P, 2048], BF16)
+            dst = gx[:].bitcast(F32).rearrange("q (a t b u) -> q a t b u", a=2, t=2, u=2)[:, a, :, :, :]
+            copy_on(e, dst, tiles["pt_%d%d%d" % (g, bh, a)][:].rearrange("q t u b -> q t b u"))
+
+        def xq(g, bh):
+            quantise("x_%d%d" % (g, bh), tiles["g_x_%d%d" % (g, bh)])
+
+        def m1(ft, bh):
+            ph = ps_h.tile([P, 512], F32, name="ph", tag="h")
+            tiles["ph_%d%d" % (ft, bh)] = ph
+            fh, r = divmod(ft, 4)
+            mx_group(
+                ph,
+                ["w1_%d%d" % (g, fh) for g in range(2)],
+                slice(P * r, P * r + P),
+                ["x_%d%d" % (g, bh) for g in range(2)],
+            )
+
+        def he(ft, bh, e):
+            g2, t = divmod(ft, 4)
+            ht = get("ht_%d%d" % (g2, bh), [P, 4, 512], BF16)
+            ph = tiles["ph_%d%d" % (ft, bh)]
+            if e == "V":
+                nc.vector.tensor_scalar(
+                    out=ht[:, t, :], in0=ph[:], scalar1=b1f[:, ft : ft + 1], scalar2=0.0, op0=ALU.add, op1=ALU.max
+                )
+            else:
+                nc.scalar.activation(out=ht[:, t, :], in_=ph[:], func=ACT.Relu, bias=b1f[:, ft : ft + 1], scale=1.0)
+
+        def hr(g2, bh, e, c0, c1):
+            regroup(e, get("g_h_%d%d" % (g2, bh), [P, 2048], BF16), tiles["ht_%d%d" % (g2, bh)][:], c0, c1)
+
+        def hq(g2, bh):
+            quantise("h_%d%d" % (g2, bh), tiles["g_h_%d%d" % (g2, bh)])
+
+        def m2(bt):
+            pv = ps_v.tile([P, M], F32, name="pv", tag="v")
+            tiles["pv_%d" % bt] = pv
+            bh, r = divmod(bt, 4)
+            mx_group(
+                pv,
+                ["h_%d%d" % (g, bh) for g in range(2)],
+                slice(P * r, P * r + P),
+                ["w2_%d" % g for g in range(2)],
+            )
+
+        def va(bt):
+            v = get("v_%d" % bt, [P, M], F32)
+            nc.vector.tensor_tensor(out=v[:], in0=tiles["pv_%d" % bt][:], in1=b2bc[:], op=ALU.add)
+
+        def sq(bt, gid, j):
+            ss = get("ss_%d" % gid, [P, 4], F32)
+            nc.scalar.activation(out=junk[:], in_=tiles["v_%d" % bt][:], func=ACT.Square, accum_out=ss[:, j : j + 1])
+
+        def tmax(gid, n):
+            ssm = get("ssm_%d" % gid, [P, 4], F32)
+            nc.vector.tensor_scalar_max(out=ssm[:, 0:n], in0=tiles["ss_%d" % gid][:, 0:n], scalar1=EPS * EPS)
+
+        def tsqrt(gid, n):
+            nrm = get("nrm_%d" % gid, [P, 4], F32)
+            nc.scalar.activation(out=nrm[:, 0:n], in_=tiles["ssm_%d" % gid][:, 0:n], func=ACT.Sqrt)
+
+        def trec(gid, n):
+            rinv = get("rinv_%d" % gid, [P, 4], F32)
+            nc.vector.reciprocal(out=rinv[:, 0:n], in_=tiles["nrm_%d" % gid][:, 0:n])
+
+        def sc(bt, e, gid, j, sid, k, n):
+            o = get("o_%d" % sid, [P, n, M], F32)
+            r = tiles["rinv_%d" % gid][:, j : j + 1]
+            v = tiles["v_%d" % bt]
+            if e == "V":
+                nc.vector.tensor_scalar_mul(out=o[:, k, :], in0=v[:], scalar1=r)
+            elif e == "S":
+                nc.scalar.activation(out=o[:, k, :], in_=v[:], func=ACT.Copy, scale=r)
+            else:
+                nc.gpsimd.tensor_scalar(out=o[:, k, :], in0=v[:], scalar1=r, scalar2=0.0, op0=ALU.mult, op1=ALU.add)
+
+        def st(sid, bt0, n):
+            nc.sync.dma_start(out=out_v[:, bt0 : bt0 + n, :], in_=tiles["o_%d" % sid][:])
+
+        steps = {
+            "ld_small": ld_small, "ld_w1r": ld_w1r, "ld_w1c": ld_w1c, "ld_x": ld_x, "ld_w2": ld_w2,
+            "sb1t": sb1t, "sb1c": sb1c, "sb2m": sb2m, "sb2c": sb2c,
+            "w1r": w1r, "w1q": w1q, "w2r": w2r, "w2q": w2q, "xt": xt, "xe": xe, "xq": xq,
+            "m1": m1, "he": he, "hr": hr, "hq": hq, "m2": m2, "va": va, "sq": sq,
+            "tmax": tmax, "tsqrt": tsqrt, "trec": trec, "sc": sc, "st": st,
+        }
+        for entry in PROGRAM:
+            steps[entry[0]](*entry[1:])

@@ -17,148 +17,175 @@ FLOPS = 2 * B * IN * F + 2 * B * F * M
 EPS = 1e-12
 
 PROGRAM = [
-    ("ld_w1r", 1, 0),
+    ("ld_x", 0),
+    ("xt", 1, 0, 0),
+    ("xt", 0, 0, 0),
+    ("xe", 1, 0, 0, "V"),
+    ("ld_w1r", 0, 1),
+    ("ld_w1r", 0, 0),
+    ("ld_x", 1),
+    ("xe", 0, 0, 0, "S"),
+    ("w1r", 0, 0, "V", 0, 256),
+    ("w1r", 0, 1, "V", 0, 256),
+    ("xt", 0, 0, 1),
+    ("w1r", 0, 0, "S", 256, 512),
+    ("w1q", 0, 0),
+    ("w1r", 0, 1, "V", 256, 512),
+    ("xe", 0, 0, 1, "S"),
     ("ld_small",),
+    ("xt", 1, 0, 1),
+    ("xe", 1, 0, 1, "S"),
+    ("sb1t",),
+    ("ld_w1r", 1, 0),
+    ("xq", 0, 0),
     ("ld_w1r", 1, 1),
     ("sb2m",),
-    ("ld_x", 0),
-    ("ld_x", 1),
+    ("sb1c", "S"),
     ("sb2c", "S"),
-    ("w1r", 1, 0, "V", 256, 512),
-    ("xt", 0, 0, 0),
-    ("xt", 0, 0, 1),
-    ("w1r", 1, 1, "S", 256, 512),
-    ("xe", 0, 0, 0, "S"),
-    ("ld_w1r", 0, 0),
-    ("w1r", 1, 1, "V", 0, 256),
-    ("ld_w1r", 0, 1),
-    ("xt", 1, 0, 1),
+    ("m1p", 0, 0, 0, 1, 0),
     ("ld_x", 2),
-    ("xe", 0, 0, 1, "S"),
-    ("xe", 1, 0, 1, "S"),
-    ("xt", 1, 0, 0),
-    ("ld_x", 3),
-    ("w1q", 1, 1),
-    ("ld_w2", 0),
-    ("w1r", 1, 0, "V", 0, 256),
-    ("w1q", 1, 0),
-    ("xq", 0, 0),
-    ("sb1t",),
-    ("xe", 1, 0, 0, "S"),
-    ("w1r", 0, 0, "S", 256, 512),
-    ("xt", 1, 1, 0),
-    ("xq", 1, 0),
-    ("ld_w2", 1),
-    ("w1r", 0, 1, "S", 256, 512),
-    ("xe", 1, 1, 0, "S"),
-    ("w1r", 0, 0, "V", 0, 256),
-    ("sb1c", "V"),
-    ("xt", 1, 1, 1),
-    ("w1q", 0, 0),
-    ("m1", 1, 0),
-    ("m1", 3, 0),
-    ("m1", 0, 0),
-    ("xt", 0, 1, 1),
-    ("w1r", 0, 1, "V", 0, 256),
     ("w1q", 0, 1),
-    ("xe", 1, 1, 1, "S"),
-    ("xq", 1, 1),
-    ("w2r", 0, "V", 256, 512),
-    ("he", 1, 0, "S"),
+    ("m1p", 2, 0, 0, 1, 0),
+    ("w1r", 1, 0, "V", 256, 512),
+    ("w1r", 1, 0, "S", 0, 256),
+    ("m1p", 1, 0, 0, 1, 0),
+    ("w1r", 1, 1, "S", 256, 512),
+    ("xq", 1, 0),
+    ("w1q", 1, 0),
+    ("m1p", 3, 0, 0, 1, 0),
+    ("xt", 1, 1, 0),
+    ("xe", 1, 1, 0, "S"),
+    ("w1r", 1, 1, "V", 0, 256),
     ("xt", 0, 1, 0),
-    ("he", 3, 0, "S"),
-    ("m1", 6, 0),
-    ("he", 0, 0, "V"),
-    ("m1", 7, 0),
+    ("m1p", 0, 0, 1, 0, 1),
     ("xe", 0, 1, 0, "V"),
-    ("xe", 0, 1, 1, "S"),
-    ("m1", 4, 0),
-    ("w2r", 1, "S", 256, 512),
-    ("w2r", 1, "V", 0, 256),
-    ("m1", 5, 0),
-    ("he", 6, 0, "S"),
-    ("xq", 0, 1),
-    ("m1", 2, 0),
-    ("he", 4, 0, "S"),
-    ("w2q", 1),
-    ("he", 7, 0, "V"),
-    ("m1", 6, 1),
-    ("w2r", 0, "V", 0, 256),
-    ("m1", 4, 1),
-    ("he", 5, 0, "S"),
-    ("hr", 1, 0, "V", 0, 256),
+    ("w1q", 1, 1),
+    ("he", 0, 0, "S"),
+    ("m1p", 1, 0, 1, 0, 1),
+    ("m1p", 3, 0, 1, 0, 1),
+    ("m1p", 2, 0, 1, 0, 1),
+    ("m1p", 6, 0, 0, 1, 0),
+    ("he", 1, 0, "S"),
+    ("he", 3, 0, "V"),
+    ("ld_x", 3),
+    ("ld_w2", 1),
     ("he", 2, 0, "S"),
-    ("w2q", 0),
-    ("he", 6, 1, "S"),
-    ("he", 4, 1, "S"),
-    ("hr", 0, 0, "V", 0, 256),
-    ("m1", 3, 1),
-    ("m1", 0, 1),
+    ("xt", 0, 1, 1),
+    ("w2r", 1, "V", 256, 512),
+    ("ld_w2", 0),
+    ("xe", 0, 1, 1, "S"),
+    ("xt", 1, 1, 1),
+    ("xe", 1, 1, 1, "S"),
+    ("m1p", 4, 0, 0, 1, 0),
+    ("m1p", 7, 0, 0, 1, 0),
+    ("w2r", 0, "S", 0, 256),
+    ("w2r", 1, "V", 0, 256),
+    ("m1p", 6, 0, 1, 0, 1),
     ("hr", 0, 0, "V", 256, 512),
-    ("m1", 5, 1),
-    ("he", 3, 1, "S"),
-    ("m1", 7, 1),
-    ("m1", 1, 1),
-    ("hr", 1, 0, "S", 256, 512),
-    ("he", 7, 1, "S"),
-    ("he", 1, 1, "S"),
-    ("he", 0, 1, "V"),
-    ("he", 5, 1, "V"),
-    ("hq", 1, 0),
-    ("m1", 2, 1),
-    ("he", 2, 1, "S"),
+    ("m1p", 4, 0, 1, 0, 1),
+    ("he", 4, 0, "S"),
+    ("m1p", 5, 0, 0, 1, 0),
+    ("xq", 0, 1),
+    ("he", 6, 0, "V"),
+    ("xq", 1, 1),
+    ("m1p", 7, 0, 1, 0, 1),
+    ("he", 7, 0, "S"),
+    ("w2r", 0, "V", 256, 512),
+    ("m1p", 0, 1, 0, 1, 0),
+    ("hr", 0, 0, "V", 0, 256),
+    ("m1p", 5, 0, 1, 0, 1),
+    ("he", 5, 0, "S"),
+    ("w2q", 0),
+    ("m1p", 2, 1, 0, 1, 0),
+    ("m1p", 0, 1, 1, 0, 1),
     ("hq", 0, 0),
-    ("hr", 1, 1, "S", 0, 256),
-    ("hr", 1, 1, "V", 256, 512),
-    ("m2", 2),
+    ("m1p", 2, 1, 1, 0, 1),
+    ("m1p", 1, 1, 0, 1, 0),
+    ("he", 0, 1, "S"),
+    ("hr", 1, 0, "V", 0, 256),
+    ("m1p", 6, 1, 0, 1, 0),
+    ("m1p", 1, 1, 1, 0, 1),
+    ("he", 2, 1, "V"),
+    ("m1p", 3, 1, 0, 1, 0),
+    ("hr", 1, 0, "S", 256, 512),
+    ("m1p", 6, 1, 1, 0, 1),
+    ("m1p", 3, 1, 1, 0, 1),
+    ("w2q", 1),
+    ("m2p", 1, 0, 1, 0),
+    ("hq", 1, 0),
+    ("m1p", 4, 1, 0, 1, 0),
+    ("he", 1, 1, "S"),
+    ("he", 3, 1, "S"),
+    ("m1p", 5, 1, 0, 1, 0),
+    ("m1p", 4, 1, 1, 0, 1),
     ("hr", 0, 1, "V", 0, 256),
-    ("va", 2),
-    ("hr", 0, 1, "S", 256, 512),
-    ("sq", 2, 0, 2),
-    ("m2", 1),
+    ("m1p", 5, 1, 1, 0, 1),
+    ("he", 6, 1, "S"),
+    ("m2p", 1, 1, 0, 1),
+    ("m1p", 7, 1, 0, 1, 0),
+    ("hr", 0, 1, "V", 256, 512),
+    ("he", 4, 1, "S"),
     ("va", 1),
-    ("hq", 1, 1),
-    ("m2", 0),
+    ("m2p", 2, 0, 1, 0),
+    ("m1p", 7, 1, 1, 0, 1),
+    ("he", 5, 1, "S"),
+    ("he", 7, 1, "S"),
+    ("m2p", 2, 1, 0, 1),
     ("hq", 0, 1),
-    ("m2", 3),
-    ("va", 0),
-    ("va", 3),
+    ("va", 2),
+    ("hr", 1, 1, "V", 0, 256),
+    ("m2p", 0, 0, 1, 0),
+    ("m2p", 0, 1, 0, 1),
+    ("hr", 1, 1, "S", 256, 512),
     ("sq", 1, 0, 1),
-    ("m2", 5),
+    ("m2p", 3, 0, 1, 0),
+    ("va", 0),
     ("sq", 0, 0, 0),
+    ("hq", 1, 1),
+    ("m2p", 3, 1, 0, 1),
+    ("m2p", 5, 0, 1, 0),
+    ("va", 3),
+    ("sq", 2, 1, 0),
+    ("tmax", 0, 2),
+    ("m2p", 5, 1, 0, 1),
+    ("tsqrt", 0, 2),
     ("va", 5),
-    ("sq", 3, 0, 3),
-    ("tmax", 0, 4),
-    ("m2", 4),
-    ("sq", 5, 1, 1),
+    ("m2p", 4, 0, 1, 0),
+    ("m2p", 4, 1, 0, 1),
+    ("trec", 0, 2),
     ("va", 4),
-    ("tsqrt", 0, 4),
-    ("m2", 6),
-    ("trec", 0, 4),
-    ("sc", 3, "V", 0, 3, 1, 1, 2),
-    ("m2", 7),
-    ("sc", 2, "V", 0, 2, 1, 0, 2),
-    ("sq", 4, 1, 0),
+    ("m2p", 6, 0, 1, 0),
+    ("sq", 3, 1, 1),
+    ("sq", 5, 2, 1),
     ("tmax", 1, 2),
-    ("va", 6),
-    ("sc", 0, "S", 0, 0, 0, 0, 2),
-    ("sc", 1, "V", 0, 1, 0, 1, 2),
+    ("m2p", 6, 1, 0, 1),
+    ("sc", 1, "G", 0, 1, 0, 1, 2),
+    ("sc", 0, "V", 0, 0, 0, 0, 2),
+    ("m2p", 7, 0, 1, 0),
     ("tsqrt", 1, 2),
-    ("sq", 6, 2, 0),
+    ("sq", 4, 2, 0),
     ("trec", 1, 2),
-    ("va", 7),
-    ("sc", 5, "V", 1, 1, 2, 1, 2),
-    ("sc", 4, "V", 1, 0, 2, 0, 2),
-    ("sq", 7, 2, 1),
-    ("st", 1, 2, 2),
+    ("sc", 2, "S", 1, 0, 1, 0, 2),
+    ("m2p", 7, 1, 0, 1),
+    ("va", 6),
+    ("sc", 3, "G", 1, 1, 1, 1, 2),
     ("tmax", 2, 2),
     ("tsqrt", 2, 2),
-    ("st", 0, 0, 2),
+    ("sq", 6, 3, 0),
+    ("va", 7),
     ("trec", 2, 2),
-    ("sc", 7, "S", 2, 1, 4, 0, 1),
-    ("sc", 6, "V", 2, 0, 3, 0, 1),
+    ("st", 0, 0, 2),
+    ("st", 1, 2, 2),
+    ("sc", 5, "V", 2, 1, 2, 1, 2),
+    ("sc", 4, "V", 2, 0, 2, 0, 2),
+    ("sq", 7, 3, 1),
+    ("tmax", 3, 2),
+    ("tsqrt", 3, 2),
     ("st", 2, 4, 2),
+    ("trec", 3, 2),
+    ("sc", 6, "V", 3, 0, 3, 0, 1),
     ("st", 3, 6, 1),
+    ("sc", 7, "V", 3, 1, 4, 0, 1),
     ("st", 4, 7, 1),
 ]
 
@@ -218,17 +245,16 @@ def tile_geometricmanifoldnetwork_pa_kernel(tc, x, W1, b1, W2, b2, out):
             scales = get("s_" + name, [P, 512], U8)
             nc.vector.quantize_mx(out=codes[:].bitcast(FP8X4), scales=scales[:], in_=src[:])
 
-        def mx_group(acc, lhs_names, lcols, rhs_names):
-            for g in range(2):
-                nc.tensor.matmul_mx(
-                    out=acc[:],
-                    lhsT=tiles["c_" + lhs_names[g]][:, lcols].bitcast(FP8X4),
-                    lhsT_scale=tiles["s_" + lhs_names[g]][:, lcols],
-                    rhs=tiles["c_" + rhs_names[g]][:].bitcast(FP8X4),
-                    rhs_scale=tiles["s_" + rhs_names[g]][:],
-                    start=(g == 0),
-                    stop=(g == 1),
-                )
+        def mx_pass(acc, lhs_name, lcols, rhs_name, start, stop):
+            nc.tensor.matmul_mx(
+                out=acc[:],
+                lhsT=tiles["c_" + lhs_name][:, lcols].bitcast(FP8X4),
+                lhsT_scale=tiles["s_" + lhs_name][:, lcols],
+                rhs=tiles["c_" + rhs_name][:].bitcast(FP8X4),
+                rhs_scale=tiles["s_" + rhs_name][:],
+                start=(start == 1),
+                stop=(stop == 1),
+            )
 
         def ld_small():
             nc.sync.dma_start(out=small[0:8, 512:640], in_=b1.rearrange("(r c) -> r c", c=P))
@@ -306,16 +332,11 @@ def tile_geometricmanifoldnetwork_pa_kernel(tc, x, W1, b1, W2, b2, out):
         def xq(g, bh):
             quantise("x_%d%d" % (g, bh), tiles["g_x_%d%d" % (g, bh)])
 
-        def m1(ft, bh):
-            ph = ps_h.tile([P, 512], F32, name="ph", tag="h")
-            tiles["ph_%d%d" % (ft, bh)] = ph
+        def m1p(ft, bh, g, start, stop):
+            if start == 1:
+                tiles["ph_%d%d" % (ft, bh)] = ps_h.tile([P, 512], F32, name="ph", tag="h")
             fh, r = divmod(ft, 4)
-            mx_group(
-                ph,
-                ["w1_%d%d" % (g, fh) for g in range(2)],
-                slice(P * r, P * r + P),
-                ["x_%d%d" % (g, bh) for g in range(2)],
-            )
+            mx_pass(tiles["ph_%d%d" % (ft, bh)], "w1_%d%d" % (g, fh), slice(P * r, P * r + P), "x_%d%d" % (g, bh), start, stop)
 
         def he(ft, bh, e):
             g2, t = divmod(ft, 4)
@@ -334,16 +355,11 @@ def tile_geometricmanifoldnetwork_pa_kernel(tc, x, W1, b1, W2, b2, out):
         def hq(g2, bh):
             quantise("h_%d%d" % (g2, bh), tiles["g_h_%d%d" % (g2, bh)])
 
-        def m2(bt):
-            pv = ps_v.tile([P, M], F32, name="pv", tag="v")
-            tiles["pv_%d" % bt] = pv
+        def m2p(bt, g, start, stop):
+            if start == 1:
+                tiles["pv_%d" % bt] = ps_v.tile([P, M], F32, name="pv", tag="v")
             bh, r = divmod(bt, 4)
-            mx_group(
-                pv,
-                ["h_%d%d" % (g, bh) for g in range(2)],
-                slice(P * r, P * r + P),
-                ["w2_%d" % g for g in range(2)],
-            )
+            mx_pass(tiles["pv_%d" % bt], "h_%d%d" % (g, bh), slice(P * r, P * r + P), "w2_%d" % g, start, stop)
 
         def va(bt):
             v = get("v_%d" % bt, [P, M], F32)
@@ -383,7 +399,7 @@ def tile_geometricmanifoldnetwork_pa_kernel(tc, x, W1, b1, W2, b2, out):
             "ld_small": ld_small, "ld_w1r": ld_w1r, "ld_w1c": ld_w1c, "ld_x": ld_x, "ld_w2": ld_w2,
             "sb1t": sb1t, "sb1c": sb1c, "sb2m": sb2m, "sb2c": sb2c,
             "w1r": w1r, "w1q": w1q, "w2r": w2r, "w2q": w2q, "xt": xt, "xe": xe, "xq": xq,
-            "m1": m1, "he": he, "hr": hr, "hq": hq, "m2": m2, "va": va, "sq": sq,
+            "m1p": m1p, "he": he, "hr": hr, "hq": hq, "m2p": m2p, "va": va, "sq": sq,
             "tmax": tmax, "tsqrt": tsqrt, "trec": trec, "sc": sc, "st": st,
         }
         for entry in PROGRAM:

@@ -12,395 +12,219 @@ ACT = mybir.ActivationFunctionType
 ALU = mybir.AluOpType
 
 P = 128
+PACK = 4
 B, IN, F, M = 1024, 1024, 1024, 512
-FLOPS = 2 * B * IN * F + 2 * B * F * M
+PASSES = 2
+WIDE = 512
+ROW_TILES = B // P
 EPS = 1e-12
+FLOPS = 2 * B * IN * F + 2 * B * F * M
 
-PROGRAM = [
-    ("ld_x", 0),
-    ("xt", 1, 0, 0),
-    ("xt", 0, 0, 0),
-    ("xe", 1, 0, 0, "V"),
-    ("ld_w1r", 0, 1),
-    ("ld_w1r", 0, 0),
-    ("ld_x", 1),
-    ("xe", 0, 0, 0, "S"),
-    ("w1r", 0, 0, "V", 0, 256),
-    ("w1r", 0, 1, "V", 0, 256),
-    ("xt", 0, 0, 1),
-    ("w1r", 0, 0, "S", 256, 512),
-    ("w1q", 0, 0),
-    ("w1r", 0, 1, "V", 256, 512),
-    ("xe", 0, 0, 1, "S"),
-    ("ld_small",),
-    ("xt", 1, 0, 1),
-    ("xe", 1, 0, 1, "S"),
-    ("sb1t",),
-    ("ld_w1r", 1, 0),
-    ("xq", 0, 0),
-    ("ld_w1r", 1, 1),
-    ("sb2m",),
-    ("sb1c", "S"),
-    ("sb2c", "S"),
-    ("m1p", 0, 0, 0, 1, 0),
-    ("ld_x", 2),
-    ("w1q", 0, 1),
-    ("m1p", 2, 0, 0, 1, 0),
-    ("w1r", 1, 0, "V", 256, 512),
-    ("w1r", 1, 0, "S", 0, 256),
-    ("m1p", 1, 0, 0, 1, 0),
-    ("w1r", 1, 1, "S", 256, 512),
-    ("xq", 1, 0),
-    ("w1q", 1, 0),
-    ("m1p", 3, 0, 0, 1, 0),
-    ("xt", 1, 1, 0),
-    ("xe", 1, 1, 0, "S"),
-    ("w1r", 1, 1, "V", 0, 256),
-    ("xt", 0, 1, 0),
-    ("m1p", 0, 0, 1, 0, 1),
-    ("xe", 0, 1, 0, "V"),
-    ("w1q", 1, 1),
-    ("he", 0, 0, "S"),
-    ("m1p", 1, 0, 1, 0, 1),
-    ("m1p", 3, 0, 1, 0, 1),
-    ("m1p", 2, 0, 1, 0, 1),
-    ("m1p", 6, 0, 0, 1, 0),
-    ("he", 1, 0, "S"),
-    ("he", 3, 0, "V"),
-    ("ld_x", 3),
-    ("ld_w2", 1),
-    ("he", 2, 0, "S"),
-    ("xt", 0, 1, 1),
-    ("w2r", 1, "V", 256, 512),
-    ("ld_w2", 0),
-    ("xe", 0, 1, 1, "S"),
-    ("xt", 1, 1, 1),
-    ("xe", 1, 1, 1, "S"),
-    ("m1p", 4, 0, 0, 1, 0),
-    ("m1p", 7, 0, 0, 1, 0),
-    ("w2r", 0, "S", 0, 256),
-    ("w2r", 1, "V", 0, 256),
-    ("m1p", 6, 0, 1, 0, 1),
-    ("hr", 0, 0, "V", 256, 512),
-    ("m1p", 4, 0, 1, 0, 1),
-    ("he", 4, 0, "S"),
-    ("m1p", 5, 0, 0, 1, 0),
-    ("xq", 0, 1),
-    ("he", 6, 0, "V"),
-    ("xq", 1, 1),
-    ("m1p", 7, 0, 1, 0, 1),
-    ("he", 7, 0, "S"),
-    ("w2r", 0, "V", 256, 512),
-    ("m1p", 0, 1, 0, 1, 0),
-    ("hr", 0, 0, "V", 0, 256),
-    ("m1p", 5, 0, 1, 0, 1),
-    ("he", 5, 0, "S"),
-    ("w2q", 0),
-    ("m1p", 2, 1, 0, 1, 0),
-    ("m1p", 0, 1, 1, 0, 1),
-    ("hq", 0, 0),
-    ("m1p", 2, 1, 1, 0, 1),
-    ("m1p", 1, 1, 0, 1, 0),
-    ("he", 0, 1, "S"),
-    ("hr", 1, 0, "V", 0, 256),
-    ("m1p", 6, 1, 0, 1, 0),
-    ("m1p", 1, 1, 1, 0, 1),
-    ("he", 2, 1, "V"),
-    ("m1p", 3, 1, 0, 1, 0),
-    ("hr", 1, 0, "S", 256, 512),
-    ("m1p", 6, 1, 1, 0, 1),
-    ("m1p", 3, 1, 1, 0, 1),
-    ("w2q", 1),
-    ("m2p", 1, 0, 1, 0),
-    ("hq", 1, 0),
-    ("m1p", 4, 1, 0, 1, 0),
-    ("he", 1, 1, "S"),
-    ("he", 3, 1, "S"),
-    ("m1p", 5, 1, 0, 1, 0),
-    ("m1p", 4, 1, 1, 0, 1),
-    ("hr", 0, 1, "V", 0, 256),
-    ("m1p", 5, 1, 1, 0, 1),
-    ("he", 6, 1, "S"),
-    ("m2p", 1, 1, 0, 1),
-    ("m1p", 7, 1, 0, 1, 0),
-    ("hr", 0, 1, "V", 256, 512),
-    ("he", 4, 1, "S"),
-    ("va", 1),
-    ("m2p", 2, 0, 1, 0),
-    ("m1p", 7, 1, 1, 0, 1),
-    ("he", 5, 1, "S"),
-    ("he", 7, 1, "S"),
-    ("m2p", 2, 1, 0, 1),
-    ("hq", 0, 1),
-    ("va", 2),
-    ("hr", 1, 1, "V", 0, 256),
-    ("m2p", 0, 0, 1, 0),
-    ("m2p", 0, 1, 0, 1),
-    ("hr", 1, 1, "S", 256, 512),
-    ("sq", 1, 0, 1),
-    ("m2p", 3, 0, 1, 0),
-    ("va", 0),
-    ("sq", 0, 0, 0),
-    ("hq", 1, 1),
-    ("m2p", 3, 1, 0, 1),
-    ("m2p", 5, 0, 1, 0),
-    ("va", 3),
-    ("sq", 2, 1, 0),
-    ("tmax", 0, 2),
-    ("m2p", 5, 1, 0, 1),
-    ("tsqrt", 0, 2),
-    ("va", 5),
-    ("m2p", 4, 0, 1, 0),
-    ("m2p", 4, 1, 0, 1),
-    ("trec", 0, 2),
-    ("va", 4),
-    ("m2p", 6, 0, 1, 0),
-    ("sq", 3, 1, 1),
-    ("sq", 5, 2, 1),
-    ("tmax", 1, 2),
-    ("m2p", 6, 1, 0, 1),
-    ("sc", 1, "G", 0, 1, 0, 1, 2),
-    ("sc", 0, "V", 0, 0, 0, 0, 2),
-    ("m2p", 7, 0, 1, 0),
-    ("tsqrt", 1, 2),
-    ("sq", 4, 2, 0),
-    ("trec", 1, 2),
-    ("sc", 2, "S", 1, 0, 1, 0, 2),
-    ("m2p", 7, 1, 0, 1),
-    ("va", 6),
-    ("sc", 3, "G", 1, 1, 1, 1, 2),
-    ("tmax", 2, 2),
-    ("tsqrt", 2, 2),
-    ("sq", 6, 3, 0),
-    ("va", 7),
-    ("trec", 2, 2),
-    ("st", 0, 0, 2),
-    ("st", 1, 2, 2),
-    ("sc", 5, "V", 2, 1, 2, 1, 2),
-    ("sc", 4, "V", 2, 0, 2, 0, 2),
-    ("sq", 7, 3, 1),
-    ("tmax", 3, 2),
-    ("tsqrt", 3, 2),
-    ("st", 2, 4, 2),
-    ("trec", 3, 2),
-    ("sc", 6, "V", 3, 0, 3, 0, 1),
-    ("st", 3, 6, 1),
-    ("sc", 7, "V", 3, 1, 4, 0, 1),
-    ("st", 4, 7, 1),
-]
+W1_VECTOR_COLS = 256
 
 
 def tile_geometricmanifoldnetwork_pa_kernel(tc, x, W1, b1, W2, b2, out):
     nc = tc.nc
     with ExitStack() as ctx:
-        sb = ctx.enter_context(tc.tile_pool(name="sb", bufs=1))
-        ps_t = ctx.enter_context(tc.psum_pool(name="ps_t", bufs=2))
-        ps_h = ctx.enter_context(tc.psum_pool(name="ps_h", bufs=4))
-        ps_v = ctx.enter_context(tc.psum_pool(name="ps_v", bufs=2))
-        ctx.enter_context(tc.manual_schedule())
+        sbuf = ctx.enter_context(tc.tile_pool(name="sbuf", bufs=1))
+        psum_t = ctx.enter_context(tc.psum_pool(name="psum_t", bufs=2))
+        psum_h = ctx.enter_context(tc.psum_pool(name="psum_h", bufs=4))
+        psum_v = ctx.enter_context(tc.psum_pool(name="psum_v", bufs=2))
 
-        tiles = {}
+        def sbuf_tile(name, shape, dtype):
+            return sbuf.tile(shape, dtype, name=name, align_bytes=64)
 
-        def get(key, shape, dtype):
-            if key not in tiles:
-                tiles[key] = sb.tile(shape, dtype, name=key, align_bytes=64)
-            return tiles[key]
-
-        x_v = x.rearrange("(p t) k -> p t k", t=8)
-        w2_v = W2.rearrange("(j p) m -> p j m", p=P)
-        out_v = out.rearrange("(p t) m -> p t m", t=8)
-
-        small = get("small", [P, 640], BF16)
-        nc.vector.memset(small[:], 0.0)
-        ones_b = get("ones_b", [P, P], BF16)
-        nc.vector.memset(ones_b[:], 1.0)
-        warm_in = get("warm_in", [P, 1], F32)
-        warm_out = get("warm_out", [P, 1], F32)
-        nc.vector.memset(warm_in[:], 1.0)
-        nc.scalar.activation(out=warm_out[:], in_=warm_in[:], func=ACT.Sqrt)
-        ident_f = get("ident_f", [P, P], F32)
-        make_identity(nc, ident_f[:])
-        ident_b = get("ident_b", [P, P], BF16)
-        nc.vector.tensor_copy(out=ident_b[:], in_=ident_f[:])
-        b1f = get("b1f", [P, 8], F32)
-        b2bc = get("b2bc", [P, M], F32)
-        junk = get("junk", [P, M], F32)
-
-        def copy_on(e, dst, src):
-            if e == "V":
-                nc.vector.tensor_copy(out=dst, in_=src)
-            else:
-                nc.scalar.copy(out=dst, in_=src)
-
-        def regroup(e, dst, src, c0, c1):
-            d = dst[:].rearrange("p (w t) -> p w t", t=4)
-            copy_on(
-                e,
-                d[:, c0:c1, :].rearrange("p (c i) t -> p c t i", i=4),
-                src[:, :, c0:c1].rearrange("p t (c i) -> p c t i", i=4),
+        def mx_operand(name):
+            return (
+                sbuf_tile(name + "_grouped", [P, PACK * WIDE], BF16),
+                sbuf_tile(name + "_codes", [P, WIDE], U32),
+                sbuf_tile(name + "_scales", [P, WIDE], U8),
             )
 
-        def quantise(name, src):
-            codes = get("c_" + name, [P, 512], U32)
-            scales = get("s_" + name, [P, 512], U8)
-            nc.vector.quantize_mx(out=codes[:].bitcast(FP8X4), scales=scales[:], in_=src[:])
+        x_raw = [sbuf_tile("x_raw%d" % j, [P, 2, IN], BF16) for j in range(ROW_TILES // 2)]
+        w1_raw = [sbuf_tile("w1_raw%d" % c, [P, PACK, F], BF16) for c in range(PASSES)]
+        w2_raw = [sbuf_tile("w2_raw%d" % c, [P, PACK, M], BF16) for c in range(PASSES)]
+        x_mx = [[mx_operand("x%d%d" % (c, half)) for half in range(2)] for c in range(PASSES)]
+        w1_mx = [[mx_operand("w1%d%d" % (c, fh)) for fh in range(2)] for c in range(PASSES)]
+        h_mx = [[mx_operand("h%d%d" % (c, half)) for half in range(2)] for c in range(PASSES)]
+        w2_mx = [mx_operand("w2%d" % c) for c in range(PASSES)]
+        h_t = [[sbuf_tile("h_t%d%d" % (c, half), [P, PACK, WIDE], BF16) for half in range(2)] for c in range(PASSES)]
+        v_sb = [sbuf_tile("v%d" % j, [P, M], F32) for j in range(ROW_TILES)]
+        out_sb = [sbuf_tile("out%d" % i, [P, 2, M], F32) for i in range(ROW_TILES // 2)]
+        sumsq = [sbuf_tile("sumsq%d" % i, [P, 2], F32) for i in range(ROW_TILES // 2)]
+        floored = [sbuf_tile("floored%d" % i, [P, 2], F32) for i in range(ROW_TILES // 2)]
+        norm = [sbuf_tile("norm%d" % i, [P, 2], F32) for i in range(ROW_TILES // 2)]
+        inv_norm = [sbuf_tile("inv_norm%d" % i, [P, 2], F32) for i in range(ROW_TILES // 2)]
+        squares = sbuf_tile("squares", [P, M], F32)
 
-        def mx_pass(acc, lhs_name, lcols, rhs_name, start, stop):
+        x_view = x.rearrange("(p j) k -> p j k", j=ROW_TILES)
+        w2_view = W2.rearrange("(r p) m -> p r m", p=P)
+        out_view = out.rearrange("(p j) m -> p j m", j=ROW_TILES)
+
+        def load_x(i):
+            nc.sync.dma_start(out=x_raw[i][:], in_=x_view[:, 2 * i : 2 * i + 2, :])
+
+        def load_w1(c):
+            for u in range(2):
+                k0 = 512 * c + 256 * u
+                nc.sync.dma_start(
+                    out=w1_raw[c][:, 2 * u : 2 * u + 2, :],
+                    in_=W1[k0 : k0 + 256, :].rearrange("(q e) f -> q e f", e=2),
+                )
+
+        bias_rows = sbuf_tile("bias_rows", [P, M + P], BF16)
+        nc.vector.memset(bias_rows[:], 0.0)
+        load_x(0)
+        load_w1(0)
+        load_x(1)
+        load_w1(1)
+        nc.sync.dma_start(out=bias_rows[0 : F // P, M : M + P], in_=b1.rearrange("(r p) -> r p", p=P))
+        nc.sync.dma_start(out=bias_rows[0:1, 0:M], in_=b2.rearrange("(o m) -> o m", o=1))
+        load_x(2)
+        load_x(3)
+        for c in range(PASSES):
+            nc.sync.dma_start(out=w2_raw[c][:], in_=w2_view[:, PACK * c : PACK * c + PACK, :])
+
+        ones = sbuf_tile("ones", [P, P], BF16)
+        nc.vector.memset(ones[:], 1.0)
+        dummy_in = sbuf_tile("dummy_in", [P, 1], F32)
+        dummy_out = sbuf_tile("dummy_out", [P, 1], F32)
+        nc.vector.memset(dummy_in[:], 1.0)
+        nc.scalar.activation(out=dummy_out[:], in_=dummy_in[:], func=ACT.Sqrt)
+        identity_f32 = sbuf_tile("identity_f32", [P, P], F32)
+        make_identity(nc, identity_f32[:])
+        identity_bf16 = sbuf_tile("identity_bf16", [P, P], BF16)
+        nc.vector.tensor_copy(out=identity_bf16[:], in_=identity_f32[:])
+        b1_col = sbuf_tile("b1_col", [P, F // P], F32)
+        b2_all = sbuf_tile("b2_all", [P, M], F32)
+
+        def biases():
+            b1_ps = psum_t.tile([P, P], BF16, name="b1_ps", tag="t")
+            nc.tensor.transpose(out=b1_ps[:], in_=bias_rows[:, M : M + P], identity=identity_bf16[:])
+            nc.scalar.copy(out=b1_col[:], in_=b1_ps[:, 0 : F // P])
+            b2_ps = psum_v.tile([P, M], F32, name="b2_ps", tag="v")
+            nc.tensor.matmul(out=b2_ps[:], lhsT=ones[:], rhs=bias_rows[:, 0:M], start=True, stop=True)
+            nc.scalar.copy(out=b2_all[:], in_=b2_ps[:])
+
+        def regroup(operand, rows, vector_cols):
+            grouped = operand[0][:].rearrange("p (w t) -> p w t", t=PACK)
+            nc.vector.tensor_copy(
+                out=grouped[:, 0:vector_cols, :].rearrange("p (r i) t -> p r t i", i=4),
+                in_=rows[:, :, 0:vector_cols].rearrange("p t (r i) -> p r t i", i=4),
+            )
+            if vector_cols < WIDE:
+                nc.scalar.copy(
+                    out=grouped[:, vector_cols:WIDE, :].rearrange("p (r i) t -> p r t i", i=4),
+                    in_=rows[:, :, vector_cols:WIDE].rearrange("p t (r i) -> p r t i", i=4),
+                )
+
+        def quantise(operand):
+            grouped, codes, scales = operand
+            nc.vector.quantize_mx(out=codes[:].bitcast(FP8X4), scales=scales[:], in_=grouped[:])
+
+        def mx_pass(acc, stationary, cols, moving, c):
             nc.tensor.matmul_mx(
                 out=acc[:],
-                lhsT=tiles["c_" + lhs_name][:, lcols].bitcast(FP8X4),
-                lhsT_scale=tiles["s_" + lhs_name][:, lcols],
-                rhs=tiles["c_" + rhs_name][:].bitcast(FP8X4),
-                rhs_scale=tiles["s_" + rhs_name][:],
-                start=(start == 1),
-                stop=(stop == 1),
+                lhsT=stationary[1][:, cols].bitcast(FP8X4),
+                lhsT_scale=stationary[2][:, cols],
+                rhs=moving[1][:].bitcast(FP8X4),
+                rhs_scale=moving[2][:],
+                start=(c == 0),
+                stop=(c == PASSES - 1),
             )
 
-        def ld_small():
-            nc.sync.dma_start(out=small[0:8, 512:640], in_=b1.rearrange("(r c) -> r c", c=P))
-            nc.sync.dma_start(out=small[0:1, 0:512], in_=b2.rearrange("(o m) -> o m", o=1))
+        def x_pair(half, a):
+            words = x_raw[2 * half + a][:].rearrange("p j k -> p (j k)").bitcast(F32)
+            for c in range(PASSES):
+                x_ps = psum_t.tile([P, 2, 2, P], F32, name="x_ps", tag="t")
+                for j in range(2):
+                    for u in range(2):
+                        w0 = (IN // 2) * j + 256 * c + P * u
+                        nc.tensor.transpose(out=x_ps[:, j, u, :], in_=words[:, w0 : w0 + P], identity=identity_f32[:])
+                grouped = x_mx[c][half][0][:].bitcast(F32).rearrange("q (a j b u) -> q a j b u", a=2, j=2, u=2)
+                nc.scalar.copy(out=grouped[:, a, :, :, :], in_=x_ps[:].rearrange("q j u b -> q j b u"))
 
-        def ld_w1r(g, u):
-            raw = get("raw1_%d" % g, [P, 4, F], BF16)
-            r0 = 512 * g + 256 * u
-            nc.sync.dma_start(
-                out=raw[:, 2 * u : 2 * u + 2, :], in_=W1[r0 : r0 + 256, :].rearrange("(q e) f -> q e f", e=2)
-            )
+        def w1_pass(c):
+            for fh in range(2):
+                regroup(w1_mx[c][fh], w1_raw[c][:, :, WIDE * fh : WIDE * fh + WIDE], W1_VECTOR_COLS)
+            for fh in range(2):
+                quantise(w1_mx[c][fh])
 
-        def ld_w1c(g, fh, u):
-            raw = get("raw1_%d%d" % (g, fh), [P, 4, 512], BF16)
-            r0 = 512 * g + 256 * u
-            nc.sync.dma_start(
-                out=raw[:, 2 * u : 2 * u + 2, :],
-                in_=W1[r0 : r0 + 256, 512 * fh : 512 * fh + 512].rearrange("(q e) f -> q e f", e=2),
-            )
+        h_ps = {}
 
-        def ld_x(j):
-            xp = get("x_%d" % j, [P, 2, IN], BF16)
-            nc.sync.dma_start(out=xp[:], in_=x_v[:, 2 * j : 2 * j + 2, :])
-
-        def ld_w2(g):
-            raw = get("raw2_%d" % g, [P, 4, M], BF16)
-            nc.sync.dma_start(out=raw[:], in_=w2_v[:, 4 * g : 4 * g + 4, :])
-
-        def sb1t():
-            pb = ps_t.tile([P, P], BF16, name="pb", tag="t")
-            tiles["pb"] = pb
-            nc.tensor.transpose(out=pb[:], in_=small[:, 512:640], identity=ident_b[:])
-
-        def sb1c(e):
-            copy_on(e, b1f[:], tiles["pb"][:, 0:8])
-
-        def sb2m():
-            pb2 = ps_v.tile([P, M], F32, name="pb2", tag="v")
-            tiles["pb2"] = pb2
-            nc.tensor.matmul(out=pb2[:], lhsT=ones_b[:], rhs=small[:, 0:512], start=True, stop=True)
-
-        def sb2c(e):
-            copy_on(e, b2bc[:], tiles["pb2"][:])
-
-        def w1r(g, fh, e, c0, c1):
-            if ("raw1_%d%d" % (g, fh)) in tiles:
-                src = tiles["raw1_%d%d" % (g, fh)][:]
-            else:
-                src = tiles["raw1_%d" % g][:, :, 512 * fh : 512 * fh + 512]
-            regroup(e, get("g_w1_%d%d" % (g, fh), [P, 2048], BF16), src, c0, c1)
-
-        def w1q(g, fh):
-            quantise("w1_%d%d" % (g, fh), tiles["g_w1_%d%d" % (g, fh)])
-
-        def w2r(g, e, c0, c1):
-            regroup(e, get("g_w2_%d" % g, [P, 2048], BF16), tiles["raw2_%d" % g][:], c0, c1)
-
-        def w2q(g):
-            quantise("w2_%d" % g, tiles["g_w2_%d" % g])
-
-        def xt(g, bh, a):
-            pt = ps_t.tile([P, 2, 2, P], F32, name="pt", tag="t")
-            tiles["pt_%d%d%d" % (g, bh, a)] = pt
-            x_w = tiles["x_%d" % (2 * bh + a)][:].rearrange("p t k -> p (t k)").bitcast(F32)
-            for t in range(2):
-                for u in range(2):
-                    c0 = 512 * t + 256 * g + 128 * u
-                    nc.tensor.transpose(out=pt[:, t, u, :], in_=x_w[:, c0 : c0 + 128], identity=ident_f[:])
-
-        def xe(g, bh, a, e):
-            gx = get("g_x_%d%d" % (g, bh), [P, 2048], BF16)
-            dst = gx[:].bitcast(F32).rearrange("q (a t b u) -> q a t b u", a=2, t=2, u=2)[:, a, :, :, :]
-            copy_on(e, dst, tiles["pt_%d%d%d" % (g, bh, a)][:].rearrange("q t u b -> q t b u"))
-
-        def xq(g, bh):
-            quantise("x_%d%d" % (g, bh), tiles["g_x_%d%d" % (g, bh)])
-
-        def m1p(ft, bh, g, start, stop):
-            if start == 1:
-                tiles["ph_%d%d" % (ft, bh)] = ps_h.tile([P, 512], F32, name="ph", tag="h")
+        def mm1_pass(ft, half, c):
+            if c == 0:
+                h_ps[(ft, half)] = psum_h.tile([P, WIDE], F32, name="h_ps", tag="h")
             fh, r = divmod(ft, 4)
-            mx_pass(tiles["ph_%d%d" % (ft, bh)], "w1_%d%d" % (g, fh), slice(P * r, P * r + P), "x_%d%d" % (g, bh), start, stop)
+            mx_pass(h_ps[(ft, half)], w1_mx[c][fh], slice(P * r, P * r + P), x_mx[c][half], c)
 
-        def he(ft, bh, e):
-            g2, t = divmod(ft, 4)
-            ht = get("ht_%d%d" % (g2, bh), [P, 4, 512], BF16)
-            ph = tiles["ph_%d%d" % (ft, bh)]
-            if e == "V":
-                nc.vector.tensor_scalar(
-                    out=ht[:, t, :], in0=ph[:], scalar1=b1f[:, ft : ft + 1], scalar2=0.0, op0=ALU.add, op1=ALU.max
-                )
-            else:
-                nc.scalar.activation(out=ht[:, t, :], in_=ph[:], func=ACT.Relu, bias=b1f[:, ft : ft + 1], scale=1.0)
+        def relu(ft, half):
+            c, t = divmod(ft, PACK)
+            nc.scalar.activation(
+                out=h_t[c][half][:, t, :], in_=h_ps[(ft, half)][:], func=ACT.Relu, bias=b1_col[:, ft : ft + 1], scale=1.0
+            )
 
-        def hr(g2, bh, e, c0, c1):
-            regroup(e, get("g_h_%d%d" % (g2, bh), [P, 2048], BF16), tiles["ht_%d%d" % (g2, bh)][:], c0, c1)
+        def h_pass(c, half):
+            regroup(h_mx[c][half], h_t[c][half][:], WIDE)
+            quantise(h_mx[c][half])
 
-        def hq(g2, bh):
-            quantise("h_%d%d" % (g2, bh), tiles["g_h_%d%d" % (g2, bh)])
+        def w2_passes():
+            for c in range(PASSES):
+                regroup(w2_mx[c], w2_raw[c][:], WIDE)
+            for c in range(PASSES):
+                quantise(w2_mx[c])
 
-        def m2p(bt, g, start, stop):
-            if start == 1:
-                tiles["pv_%d" % bt] = ps_v.tile([P, M], F32, name="pv", tag="v")
-            bh, r = divmod(bt, 4)
-            mx_pass(tiles["pv_%d" % bt], "h_%d%d" % (g, bh), slice(P * r, P * r + P), "w2_%d" % g, start, stop)
+        def v_pair(i):
+            for k in range(2):
+                j = 2 * i + k
+                half, r = divmod(j, 4)
+                v_ps = psum_v.tile([P, M], F32, name="v_ps", tag="v")
+                for c in range(PASSES):
+                    mx_pass(v_ps, h_mx[c][half], slice(P * r, P * r + P), w2_mx[c], c)
+                nc.vector.tensor_tensor(out=v_sb[j][:], in0=v_ps[:], in1=b2_all[:], op=ALU.add)
+                nc.scalar.activation(out=squares[:], in_=v_sb[j][:], func=ACT.Square, accum_out=sumsq[i][:, k : k + 1])
 
-        def va(bt):
-            v = get("v_%d" % bt, [P, M], F32)
-            nc.vector.tensor_tensor(out=v[:], in0=tiles["pv_%d" % bt][:], in1=b2bc[:], op=ALU.add)
+        def normalise_pair(i):
+            nc.vector.tensor_scalar_max(out=floored[i][:], in0=sumsq[i][:], scalar1=EPS * EPS)
+            nc.scalar.activation(out=norm[i][:], in_=floored[i][:], func=ACT.Sqrt)
+            nc.vector.reciprocal(out=inv_norm[i][:], in_=norm[i][:])
+            for k in range(2):
+                nc.vector.tensor_scalar_mul(out=out_sb[i][:, k, :], in0=v_sb[2 * i + k][:], scalar1=inv_norm[i][:, k : k + 1])
+            nc.sync.dma_start(out=out_view[:, 2 * i : 2 * i + 2, :], in_=out_sb[i][:])
 
-        def sq(bt, gid, j):
-            ss = get("ss_%d" % gid, [P, 4], F32)
-            nc.scalar.activation(out=junk[:], in_=tiles["v_%d" % bt][:], func=ACT.Square, accum_out=ss[:, j : j + 1])
-
-        def tmax(gid, n):
-            ssm = get("ssm_%d" % gid, [P, 4], F32)
-            nc.vector.tensor_scalar_max(out=ssm[:, 0:n], in0=tiles["ss_%d" % gid][:, 0:n], scalar1=EPS * EPS)
-
-        def tsqrt(gid, n):
-            nrm = get("nrm_%d" % gid, [P, 4], F32)
-            nc.scalar.activation(out=nrm[:, 0:n], in_=tiles["ssm_%d" % gid][:, 0:n], func=ACT.Sqrt)
-
-        def trec(gid, n):
-            rinv = get("rinv_%d" % gid, [P, 4], F32)
-            nc.vector.reciprocal(out=rinv[:, 0:n], in_=tiles["nrm_%d" % gid][:, 0:n])
-
-        def sc(bt, e, gid, j, sid, k, n):
-            o = get("o_%d" % sid, [P, n, M], F32)
-            r = tiles["rinv_%d" % gid][:, j : j + 1]
-            v = tiles["v_%d" % bt]
-            if e == "V":
-                nc.vector.tensor_scalar_mul(out=o[:, k, :], in0=v[:], scalar1=r)
-            elif e == "S":
-                nc.scalar.activation(out=o[:, k, :], in_=v[:], func=ACT.Copy, scale=r)
-            else:
-                nc.gpsimd.tensor_scalar(out=o[:, k, :], in0=v[:], scalar1=r, scalar2=0.0, op0=ALU.mult, op1=ALU.add)
-
-        def st(sid, bt0, n):
-            nc.sync.dma_start(out=out_v[:, bt0 : bt0 + n, :], in_=tiles["o_%d" % sid][:])
-
-        steps = {
-            "ld_small": ld_small, "ld_w1r": ld_w1r, "ld_w1c": ld_w1c, "ld_x": ld_x, "ld_w2": ld_w2,
-            "sb1t": sb1t, "sb1c": sb1c, "sb2m": sb2m, "sb2c": sb2c,
-            "w1r": w1r, "w1q": w1q, "w2r": w2r, "w2q": w2q, "xt": xt, "xe": xe, "xq": xq,
-            "m1p": m1p, "he": he, "hr": hr, "hq": hq, "m2p": m2p, "va": va, "sq": sq,
-            "tmax": tmax, "tsqrt": tsqrt, "trec": trec, "sc": sc, "st": st,
-        }
-        for entry in PROGRAM:
-            steps[entry[0]](*entry[1:])
+        x_pair(0, 0)
+        w1_pass(0)
+        x_pair(0, 1)
+        for c in range(PASSES):
+            quantise(x_mx[c][0])
+        for ft in range(4):
+            mm1_pass(ft, 0, 0)
+        w1_pass(1)
+        biases()
+        for ft in range(4):
+            mm1_pass(ft, 0, 1)
+            relu(ft, 0)
+        x_pair(1, 0)
+        x_pair(1, 1)
+        for c in range(PASSES):
+            quantise(x_mx[c][1])
+        for ft in range(4, 8):
+            for c in range(PASSES):
+                mm1_pass(ft, 0, c)
+            relu(ft, 0)
+        for c in range(PASSES):
+            h_pass(c, 0)
+        w2_passes()
+        for ft in range(8):
+            for c in range(PASSES):
+                mm1_pass(ft, 1, c)
+            relu(ft, 1)
+            if ft % PACK == PACK - 1:
+                h_pass(ft // PACK, 1)
+        for i in range(2):
+            v_pair(i)
+            normalise_pair(i)
+        v_pair(2)
+        v_pair(3)
+        normalise_pair(2)
+        normalise_pair(3)

@@ -50,7 +50,7 @@ def tile_geometricmanifoldnetwork_pa_kernel(tc, x, W1, b1, W2, b2, out):
         w2_mx = [mx_operand("w2%d" % c) for c in range(PASSES)]
         h_t = [[sbuf_tile("h_t%d%d" % (c, half), [P, PACK, WIDE], BF16) for half in range(2)] for c in range(PASSES)]
         v_sb = [sbuf_tile("v%d" % j, [P, M], F32) for j in range(ROW_TILES)]
-        out_sb = [sbuf_tile("out%d" % i, [P, 2, M], F32) for i in range(ROW_TILES // 2)]
+        out_sb = [sbuf_tile("out%d" % j, [P, M], F32) for j in range(ROW_TILES)]
         sumsq = [sbuf_tile("sumsq%d" % i, [P, 2], F32) for i in range(ROW_TILES // 2)]
         floored = [sbuf_tile("floored%d" % i, [P, 2], F32) for i in range(ROW_TILES // 2)]
         norm = [sbuf_tile("norm%d" % i, [P, 2], F32) for i in range(ROW_TILES // 2)]
@@ -178,7 +178,10 @@ def tile_geometricmanifoldnetwork_pa_kernel(tc, x, W1, b1, W2, b2, out):
             for k in range(2):
                 j = 2 * i + k
                 half, r = divmod(j, 4)
-                v_ps = psum_v.tile([P, M], F32, name="v_ps", tag="v")
+                if half == 0:
+                    v_ps = psum_v.tile([P, M], F32, name="v_ps", tag="v")
+                else:
+                    v_ps = psum_h.tile([P, M], F32, name="v_ps_late", tag="h")
                 for c in range(PASSES):
                     mx_pass(v_ps, h_mx[c][half], slice(P * r, P * r + P), w2_mx[c], c)
                 nc.vector.tensor_tensor(out=v_sb[j][:], in0=v_ps[:], in1=b2_all[:], op=ALU.add)
@@ -189,8 +192,9 @@ def tile_geometricmanifoldnetwork_pa_kernel(tc, x, W1, b1, W2, b2, out):
             nc.scalar.activation(out=norm[i][:], in_=floored[i][:], func=ACT.Sqrt)
             nc.vector.reciprocal(out=inv_norm[i][:], in_=norm[i][:])
             for k in range(2):
-                nc.vector.tensor_scalar_mul(out=out_sb[i][:, k, :], in0=v_sb[2 * i + k][:], scalar1=inv_norm[i][:, k : k + 1])
-            nc.sync.dma_start(out=out_view[:, 2 * i : 2 * i + 2, :], in_=out_sb[i][:])
+                j = 2 * i + k
+                nc.vector.tensor_scalar_mul(out=out_sb[j][:], in0=v_sb[j][:], scalar1=inv_norm[i][:, k : k + 1])
+                nc.sync.dma_start(out=out_view[:, j, :], in_=out_sb[j][:])
 
         x_pair(0, 0)
         w1_pass(0)

@@ -11,16 +11,23 @@ FP8X4 = mybir.dt.float8_e4m3fn_x4
 ACT = mybir.ActivationFunctionType
 ALU = mybir.AluOpType
 
+B, IN, F, M = 1024, 1024, 1024, 512
+FLOPS = 2 * B * IN * F + 2 * B * F * M
+EPS = 1e-12
+
 P = 128
 PACK = 4
-B, IN, F, M = 1024, 1024, 1024, 512
-PASSES = 2
+K_PASS = P * PACK
+PASSES = IN // K_PASS
 WIDE = 512
+PARTS = WIDE // P
 ROW_TILES = B // P
-EPS = 1e-12
-FLOPS = 2 * B * IN * F + 2 * B * F * M
+FEATURE_TILES = F // P
+PAIRS = ROW_TILES // 2
+RUN = 4
+H_BANKS = 4
 
-W1_VECTOR_COLS = 256
+W1_VECTOR_COLS = 320
 
 
 def tile_geometricmanifoldnetwork_pa_kernel(tc, x, W1, b1, W2, b2, out):
@@ -28,7 +35,7 @@ def tile_geometricmanifoldnetwork_pa_kernel(tc, x, W1, b1, W2, b2, out):
     with ExitStack() as ctx:
         sbuf = ctx.enter_context(tc.tile_pool(name="sbuf", bufs=1))
         psum_t = ctx.enter_context(tc.psum_pool(name="psum_t", bufs=2))
-        psum_h = ctx.enter_context(tc.psum_pool(name="psum_h", bufs=4))
+        psum_h = ctx.enter_context(tc.psum_pool(name="psum_h", bufs=H_BANKS))
         psum_v = ctx.enter_context(tc.psum_pool(name="psum_v", bufs=2))
 
         def sbuf_tile(name, shape, dtype):
@@ -41,35 +48,38 @@ def tile_geometricmanifoldnetwork_pa_kernel(tc, x, W1, b1, W2, b2, out):
                 sbuf_tile(name + "_scales", [P, WIDE], U8),
             )
 
-        x_raw = [sbuf_tile("x_raw%d" % j, [P, 2, IN], BF16) for j in range(ROW_TILES // 2)]
+        x_raw = [sbuf_tile("x_raw%d" % i, [P, 2, IN], BF16) for i in range(PAIRS)]
         w1_raw = [sbuf_tile("w1_raw%d" % c, [P, PACK, F], BF16) for c in range(PASSES)]
         w2_raw = [sbuf_tile("w2_raw%d" % c, [P, PACK, M], BF16) for c in range(PASSES)]
-        x_mx = [[mx_operand("x%d%d" % (c, half)) for half in range(2)] for c in range(PASSES)]
-        w1_mx = [[mx_operand("w1%d%d" % (c, fh)) for fh in range(2)] for c in range(PASSES)]
-        h_mx = [[mx_operand("h%d%d" % (c, half)) for half in range(2)] for c in range(PASSES)]
+        x_mx = [[mx_operand("x%d%d" % (c, half)) for half in range(B // WIDE)] for c in range(PASSES)]
+        w1_mx = [[mx_operand("w1%d%d" % (c, fh)) for fh in range(F // WIDE)] for c in range(PASSES)]
+        h_mx = [[mx_operand("h%d%d" % (c, half)) for half in range(B // WIDE)] for c in range(PASSES)]
         w2_mx = [mx_operand("w2%d" % c) for c in range(PASSES)]
-        h_t = [[sbuf_tile("h_t%d%d" % (c, half), [P, PACK, WIDE], BF16) for half in range(2)] for c in range(PASSES)]
+        h_t = [
+            [sbuf_tile("h_t%d%d" % (c, half), [P, PACK, WIDE], BF16) for half in range(B // WIDE)]
+            for c in range(PASSES)
+        ]
         v_sb = [sbuf_tile("v%d" % j, [P, M], F32) for j in range(ROW_TILES)]
         out_sb = [sbuf_tile("out%d" % j, [P, M], F32) for j in range(ROW_TILES)]
-        sumsq = [sbuf_tile("sumsq%d" % i, [P, 2], F32) for i in range(ROW_TILES // 2)]
-        floored = [sbuf_tile("floored%d" % i, [P, 2], F32) for i in range(ROW_TILES // 2)]
-        norm = [sbuf_tile("norm%d" % i, [P, 2], F32) for i in range(ROW_TILES // 2)]
-        inv_norm = [sbuf_tile("inv_norm%d" % i, [P, 2], F32) for i in range(ROW_TILES // 2)]
+        sumsq = [sbuf_tile("sumsq%d" % i, [P, 2], F32) for i in range(PAIRS)]
+        floored = [sbuf_tile("floored%d" % i, [P, 2], F32) for i in range(PAIRS)]
+        norm = [sbuf_tile("norm%d" % i, [P, 2], F32) for i in range(PAIRS)]
+        inv_norm = [sbuf_tile("inv_norm%d" % i, [P, 2], F32) for i in range(PAIRS)]
         squares = sbuf_tile("squares", [P, M], F32)
 
-        x_view = x.rearrange("(p j) k -> p j k", j=ROW_TILES)
-        w2_view = W2.rearrange("(r p) m -> p r m", p=P)
-        out_view = out.rearrange("(p j) m -> p j m", j=ROW_TILES)
+        x_view = x.rearrange("(n j) k -> n j k", j=ROW_TILES)
+        w2_view = W2.rearrange("(ft p) m -> p ft m", p=P)
+        out_view = out.rearrange("(n j) m -> n j m", j=ROW_TILES)
 
         def load_x(i):
             nc.sync.dma_start(out=x_raw[i][:], in_=x_view[:, 2 * i : 2 * i + 2, :])
 
         def load_w1(c):
             for u in range(2):
-                k0 = 512 * c + 256 * u
+                k0 = K_PASS * c + 2 * P * u
                 nc.sync.dma_start(
                     out=w1_raw[c][:, 2 * u : 2 * u + 2, :],
-                    in_=W1[k0 : k0 + 256, :].rearrange("(q e) f -> q e f", e=2),
+                    in_=W1[k0 : k0 + 2 * P, :].rearrange("(q e) f -> q e f", e=2),
                 )
 
         bias_rows = sbuf_tile("bias_rows", [P, M + P], BF16)
@@ -78,7 +88,7 @@ def tile_geometricmanifoldnetwork_pa_kernel(tc, x, W1, b1, W2, b2, out):
         load_w1(0)
         load_x(1)
         load_w1(1)
-        nc.sync.dma_start(out=bias_rows[0 : F // P, M : M + P], in_=b1.rearrange("(r p) -> r p", p=P))
+        nc.sync.dma_start(out=bias_rows[0:FEATURE_TILES, M : M + P], in_=b1.rearrange("(ft p) -> ft p", p=P))
         nc.sync.dma_start(out=bias_rows[0:1, 0:M], in_=b2.rearrange("(o m) -> o m", o=1))
         load_x(2)
         load_x(3)
@@ -95,13 +105,13 @@ def tile_geometricmanifoldnetwork_pa_kernel(tc, x, W1, b1, W2, b2, out):
         make_identity(nc, identity_f32[:])
         identity_bf16 = sbuf_tile("identity_bf16", [P, P], BF16)
         nc.vector.tensor_copy(out=identity_bf16[:], in_=identity_f32[:])
-        b1_col = sbuf_tile("b1_col", [P, F // P], F32)
+        b1_col = sbuf_tile("b1_col", [P, FEATURE_TILES], F32)
         b2_all = sbuf_tile("b2_all", [P, M], F32)
 
         def biases():
             b1_ps = psum_t.tile([P, P], BF16, name="b1_ps", tag="t")
             nc.tensor.transpose(out=b1_ps[:], in_=bias_rows[:, M : M + P], identity=identity_bf16[:])
-            nc.scalar.copy(out=b1_col[:], in_=b1_ps[:, 0 : F // P])
+            nc.scalar.copy(out=b1_col[:], in_=b1_ps[:, 0:FEATURE_TILES])
             b2_ps = psum_v.tile([P, M], F32, name="b2_ps", tag="v")
             nc.tensor.matmul(out=b2_ps[:], lhsT=ones[:], rhs=bias_rows[:, 0:M], start=True, stop=True)
             nc.scalar.copy(out=b2_all[:], in_=b2_ps[:])
@@ -109,20 +119,21 @@ def tile_geometricmanifoldnetwork_pa_kernel(tc, x, W1, b1, W2, b2, out):
         def regroup(operand, rows, vector_cols):
             grouped = operand[0][:].rearrange("p (w t) -> p w t", t=PACK)
             nc.vector.tensor_copy(
-                out=grouped[:, 0:vector_cols, :].rearrange("p (r i) t -> p r t i", i=4),
-                in_=rows[:, :, 0:vector_cols].rearrange("p t (r i) -> p r t i", i=4),
+                out=grouped[:, 0:vector_cols, :].rearrange("p (g l) t -> p g t l", l=RUN),
+                in_=rows[:, :, 0:vector_cols].rearrange("p t (g l) -> p g t l", l=RUN),
             )
             if vector_cols < WIDE:
                 nc.scalar.copy(
-                    out=grouped[:, vector_cols:WIDE, :].rearrange("p (r i) t -> p r t i", i=4),
-                    in_=rows[:, :, vector_cols:WIDE].rearrange("p t (r i) -> p r t i", i=4),
+                    out=grouped[:, vector_cols:WIDE, :].rearrange("p (g l) t -> p g t l", l=RUN),
+                    in_=rows[:, :, vector_cols:WIDE].rearrange("p t (g l) -> p g t l", l=RUN),
                 )
 
         def quantise(operand):
             grouped, codes, scales = operand
             nc.vector.quantize_mx(out=codes[:].bitcast(FP8X4), scales=scales[:], in_=grouped[:])
 
-        def mx_pass(acc, stationary, cols, moving, c):
+        def mx_pass(acc, stationary, part, moving, c):
+            cols = slice(P * part, P * part + P)
             nc.tensor.matmul_mx(
                 out=acc[:],
                 lhsT=stationary[1][:, cols].bitcast(FP8X4),
@@ -133,21 +144,22 @@ def tile_geometricmanifoldnetwork_pa_kernel(tc, x, W1, b1, W2, b2, out):
                 stop=(c == PASSES - 1),
             )
 
-        def x_pair(half, a):
-            words = x_raw[2 * half + a][:].rearrange("p j k -> p (j k)").bitcast(F32)
+        def x_pair(i):
+            half, a = divmod(i, 2)
+            words = x_raw[i][:].rearrange("n s k -> n (s k)").bitcast(F32)
             for c in range(PASSES):
                 x_ps = psum_t.tile([P, 2, 2, P], F32, name="x_ps", tag="t")
-                for j in range(2):
+                for s in range(2):
                     for u in range(2):
-                        w0 = (IN // 2) * j + 256 * c + P * u
-                        nc.tensor.transpose(out=x_ps[:, j, u, :], in_=words[:, w0 : w0 + P], identity=identity_f32[:])
-                grouped = x_mx[c][half][0][:].bitcast(F32).rearrange("q (a j b u) -> q a j b u", a=2, j=2, u=2)
-                nc.scalar.copy(out=grouped[:, a, :, :, :], in_=x_ps[:].rearrange("q j u b -> q j b u"))
+                        w0 = (IN // 2) * s + (K_PASS // 2) * c + P * u
+                        nc.tensor.transpose(out=x_ps[:, s, u, :], in_=words[:, w0 : w0 + P], identity=identity_f32[:])
+                grouped = x_mx[c][half][0][:].bitcast(F32).rearrange("q (a s n u) -> q a s n u", a=2, s=2, u=2)
+                nc.scalar.copy(out=grouped[:, a, :, :, :], in_=x_ps[:].rearrange("q s u n -> q s n u"))
 
         def w1_pass(c):
-            for fh in range(2):
+            for fh in range(F // WIDE):
                 regroup(w1_mx[c][fh], w1_raw[c][:, :, WIDE * fh : WIDE * fh + WIDE], W1_VECTOR_COLS)
-            for fh in range(2):
+            for fh in range(F // WIDE):
                 quantise(w1_mx[c][fh])
 
         h_ps = {}
@@ -155,13 +167,17 @@ def tile_geometricmanifoldnetwork_pa_kernel(tc, x, W1, b1, W2, b2, out):
         def mm1_pass(ft, half, c):
             if c == 0:
                 h_ps[(ft, half)] = psum_h.tile([P, WIDE], F32, name="h_ps", tag="h")
-            fh, r = divmod(ft, 4)
-            mx_pass(h_ps[(ft, half)], w1_mx[c][fh], slice(P * r, P * r + P), x_mx[c][half], c)
+            fh, part = divmod(ft, PARTS)
+            mx_pass(h_ps[(ft, half)], w1_mx[c][fh], part, x_mx[c][half], c)
 
         def relu(ft, half):
             c, t = divmod(ft, PACK)
             nc.scalar.activation(
-                out=h_t[c][half][:, t, :], in_=h_ps[(ft, half)][:], func=ACT.Relu, bias=b1_col[:, ft : ft + 1], scale=1.0
+                out=h_t[c][half][:, t, :],
+                in_=h_ps[(ft, half)][:],
+                func=ACT.Relu,
+                bias=b1_col[:, ft : ft + 1],
+                scale=1.0,
             )
 
         def h_pass(c, half):
@@ -175,51 +191,51 @@ def tile_geometricmanifoldnetwork_pa_kernel(tc, x, W1, b1, W2, b2, out):
                 quantise(w2_mx[c])
 
         def v_pair(i):
-            for k in range(2):
-                j = 2 * i + k
-                half, r = divmod(j, 4)
+            for s in range(2):
+                j = 2 * i + s
+                half, part = divmod(j, PARTS)
                 if half == 0:
                     v_ps = psum_v.tile([P, M], F32, name="v_ps", tag="v")
                 else:
                     v_ps = psum_h.tile([P, M], F32, name="v_ps_late", tag="h")
                 for c in range(PASSES):
-                    mx_pass(v_ps, h_mx[c][half], slice(P * r, P * r + P), w2_mx[c], c)
+                    mx_pass(v_ps, h_mx[c][half], part, w2_mx[c], c)
                 nc.vector.tensor_tensor(out=v_sb[j][:], in0=v_ps[:], in1=b2_all[:], op=ALU.add)
-                nc.scalar.activation(out=squares[:], in_=v_sb[j][:], func=ACT.Square, accum_out=sumsq[i][:, k : k + 1])
+                nc.scalar.activation(out=squares[:], in_=v_sb[j][:], func=ACT.Square, accum_out=sumsq[i][:, s : s + 1])
 
         def normalise_pair(i):
             nc.vector.tensor_scalar_max(out=floored[i][:], in0=sumsq[i][:], scalar1=EPS * EPS)
             nc.scalar.activation(out=norm[i][:], in_=floored[i][:], func=ACT.Sqrt)
             nc.vector.reciprocal(out=inv_norm[i][:], in_=norm[i][:])
-            for k in range(2):
-                j = 2 * i + k
-                nc.vector.tensor_scalar_mul(out=out_sb[j][:], in0=v_sb[j][:], scalar1=inv_norm[i][:, k : k + 1])
+            for s in range(2):
+                j = 2 * i + s
+                nc.vector.tensor_scalar_mul(out=out_sb[j][:], in0=v_sb[j][:], scalar1=inv_norm[i][:, s : s + 1])
                 nc.sync.dma_start(out=out_view[:, j, :], in_=out_sb[j][:])
 
-        x_pair(0, 0)
+        x_pair(0)
         w1_pass(0)
-        x_pair(0, 1)
+        x_pair(1)
         for c in range(PASSES):
             quantise(x_mx[c][0])
-        for ft in range(4):
+        for ft in range(H_BANKS):
             mm1_pass(ft, 0, 0)
         w1_pass(1)
         biases()
-        for ft in range(4):
+        for ft in range(H_BANKS):
             mm1_pass(ft, 0, 1)
             relu(ft, 0)
-        x_pair(1, 0)
-        x_pair(1, 1)
+        x_pair(2)
+        x_pair(3)
         for c in range(PASSES):
             quantise(x_mx[c][1])
-        for ft in range(4, 8):
+        for ft in range(H_BANKS, FEATURE_TILES):
             for c in range(PASSES):
                 mm1_pass(ft, 0, c)
             relu(ft, 0)
         for c in range(PASSES):
             h_pass(c, 0)
         w2_passes()
-        for ft in range(8):
+        for ft in range(FEATURE_TILES):
             for c in range(PASSES):
                 mm1_pass(ft, 1, c)
             relu(ft, 1)

from contextlib import ExitStack

import concourse.mybir as mybir
from concourse.masks import make_identity

F32 = mybir.dt.float32
BF16 = mybir.dt.bfloat16
U32 = mybir.dt.uint32
U8 = mybir.dt.uint8
FP8X4 = mybir.dt.float8_e4m3fn_x4
ACT = mybir.ActivationFunctionType
ALU = mybir.AluOpType

B, IN, F, M = 1024, 1024, 1024, 512
FLOPS = 2 * B * IN * F + 2 * B * F * M
EPS = 1e-12

P = 128
PACK = 4
K_PASS = P * PACK
PASSES = IN // K_PASS
WIDE = 512
PARTS = WIDE // P
ROW_TILES = B // P
FEATURE_TILES = F // P
PAIRS = ROW_TILES // 2
RUN = 4
H_BANKS = 4

W1_VECTOR_COLS = 320


def tile_geometricmanifoldnetwork_pa_kernel(tc, x, W1, b1, W2, b2, out):
    nc = tc.nc
    with ExitStack() as ctx:
        sbuf = ctx.enter_context(tc.tile_pool(name="sbuf", bufs=1))
        psum_t = ctx.enter_context(tc.psum_pool(name="psum_t", bufs=2))
        psum_h = ctx.enter_context(tc.psum_pool(name="psum_h", bufs=H_BANKS))
        psum_v = ctx.enter_context(tc.psum_pool(name="psum_v", bufs=2))

        def sbuf_tile(name, shape, dtype):
            return sbuf.tile(shape, dtype, name=name, align_bytes=64)

        def mx_operand(name):
            return (
                sbuf_tile(name + "_grouped", [P, PACK * WIDE], BF16),
                sbuf_tile(name + "_codes", [P, WIDE], U32),
                sbuf_tile(name + "_scales", [P, WIDE], U8),
            )

        x_raw = [sbuf_tile("x_raw%d" % i, [P, 2, IN], BF16) for i in range(PAIRS)]
        w1_raw = [sbuf_tile("w1_raw%d" % c, [P, PACK, F], BF16) for c in range(PASSES)]
        w2_raw = [sbuf_tile("w2_raw%d" % c, [P, PACK, M], BF16) for c in range(PASSES)]
        x_mx = [[mx_operand("x%d%d" % (c, half)) for half in range(B // WIDE)] for c in range(PASSES)]
        w1_mx = [[mx_operand("w1%d%d" % (c, fh)) for fh in range(F // WIDE)] for c in range(PASSES)]
        h_mx = [[mx_operand("h%d%d" % (c, half)) for half in range(B // WIDE)] for c in range(PASSES)]
        w2_mx = [mx_operand("w2%d" % c) for c in range(PASSES)]
        h_t = [
            [sbuf_tile("h_t%d%d" % (c, half), [P, PACK, WIDE], BF16) for half in range(B // WIDE)]
            for c in range(PASSES)
        ]
        v_sb = [sbuf_tile("v%d" % j, [P, M], F32) for j in range(ROW_TILES)]
        out_sb = [sbuf_tile("out%d" % j, [P, M], F32) for j in range(ROW_TILES)]
        sumsq = [sbuf_tile("sumsq%d" % i, [P, 2], F32) for i in range(PAIRS)]
        floored = [sbuf_tile("floored%d" % i, [P, 2], F32) for i in range(PAIRS)]
        norm = [sbuf_tile("norm%d" % i, [P, 2], F32) for i in range(PAIRS)]
        inv_norm = [sbuf_tile("inv_norm%d" % i, [P, 2], F32) for i in range(PAIRS)]
        squares = sbuf_tile("squares", [P, M], F32)

        x_view = x.rearrange("(n j) k -> n j k", j=ROW_TILES)
        w2_view = W2.rearrange("(ft p) m -> p ft m", p=P)
        out_view = out.rearrange("(n j) m -> n j m", j=ROW_TILES)

        def load_x(i):
            nc.sync.dma_start(out=x_raw[i][:], in_=x_view[:, 2 * i : 2 * i + 2, :])

        def load_w1(c):
            for u in range(2):
                k0 = K_PASS * c + 2 * P * u
                nc.sync.dma_start(
                    out=w1_raw[c][:, 2 * u : 2 * u + 2, :],
                    in_=W1[k0 : k0 + 2 * P, :].rearrange("(q e) f -> q e f", e=2),
                )

        bias_rows = sbuf_tile("bias_rows", [P, M + P], BF16)
        nc.vector.memset(bias_rows[:], 0.0)
        load_x(0)
        load_w1(0)
        load_x(1)
        load_w1(1)
        nc.sync.dma_start(out=bias_rows[0:FEATURE_TILES, M : M + P], in_=b1.rearrange("(ft p) -> ft p", p=P))
        nc.sync.dma_start(out=bias_rows[0:1, 0:M], in_=b2.rearrange("(o m) -> o m", o=1))
        load_x(2)
        load_x(3)
        for c in range(PASSES):
            nc.sync.dma_start(out=w2_raw[c][:], in_=w2_view[:, PACK * c : PACK * c + PACK, :])

        ones = sbuf_tile("ones", [P, P], BF16)
        nc.vector.memset(ones[:], 1.0)
        dummy_in = sbuf_tile("dummy_in", [P, 1], F32)
        dummy_out = sbuf_tile("dummy_out", [P, 1], F32)
        nc.vector.memset(dummy_in[:], 1.0)
        nc.scalar.activation(out=dummy_out[:], in_=dummy_in[:], func=ACT.Sqrt)
        identity_f32 = sbuf_tile("identity_f32", [P, P], F32)
        make_identity(nc, identity_f32[:])
        identity_bf16 = sbuf_tile("identity_bf16", [P, P], BF16)
        nc.vector.tensor_copy(out=identity_bf16[:], in_=identity_f32[:])
        b1_col = sbuf_tile("b1_col", [P, FEATURE_TILES], F32)
        b2_all = sbuf_tile("b2_all", [P, M], F32)

        def biases():
            b1_ps = psum_t.tile([P, P], BF16, name="b1_ps", tag="t")
            nc.tensor.transpose(out=b1_ps[:], in_=bias_rows[:, M : M + P], identity=identity_bf16[:])
            nc.scalar.copy(out=b1_col[:], in_=b1_ps[:, 0:FEATURE_TILES])
            b2_ps = psum_v.tile([P, M], F32, name="b2_ps", tag="v")
            nc.tensor.matmul(out=b2_ps[:], lhsT=ones[:], rhs=bias_rows[:, 0:M], start=True, stop=True)
            nc.scalar.copy(out=b2_all[:], in_=b2_ps[:])

        def regroup(operand, rows, vector_cols):
            grouped = operand[0][:].rearrange("p (w t) -> p w t", t=PACK)
            nc.vector.tensor_copy(
                out=grouped[:, 0:vector_cols, :].rearrange("p (g l) t -> p g t l", l=RUN),
                in_=rows[:, :, 0:vector_cols].rearrange("p t (g l) -> p g t l", l=RUN),
            )
            if vector_cols < WIDE:
                nc.scalar.copy(
                    out=grouped[:, vector_cols:WIDE, :].rearrange("p (g l) t -> p g t l", l=RUN),
                    in_=rows[:, :, vector_cols:WIDE].rearrange("p t (g l) -> p g t l", l=RUN),
                )

        def quantise(operand):
            grouped, codes, scales = operand
            nc.vector.quantize_mx(out=codes[:].bitcast(FP8X4), scales=scales[:], in_=grouped[:])

        def mx_pass(acc, stationary, part, moving, c):
            cols = slice(P * part, P * part + P)
            nc.tensor.matmul_mx(
                out=acc[:],
                lhsT=stationary[1][:, cols].bitcast(FP8X4),
                lhsT_scale=stationary[2][:, cols],
                rhs=moving[1][:].bitcast(FP8X4),
                rhs_scale=moving[2][:],
                start=(c == 0),
                stop=(c == PASSES - 1),
            )

        def x_pair(i):
            half, a = divmod(i, 2)
            words = x_raw[i][:].rearrange("n s k -> n (s k)").bitcast(F32)
            for c in range(PASSES):
                x_ps = psum_t.tile([P, 2, 2, P], F32, name="x_ps", tag="t")
                for s in range(2):
                    for u in range(2):
                        w0 = (IN // 2) * s + (K_PASS // 2) * c + P * u
                        nc.tensor.transpose(out=x_ps[:, s, u, :], in_=words[:, w0 : w0 + P], identity=identity_f32[:])
                grouped = x_mx[c][half][0][:].bitcast(F32).rearrange("q (a s n u) -> q a s n u", a=2, s=2, u=2)
                nc.scalar.copy(out=grouped[:, a, :, :, :], in_=x_ps[:].rearrange("q s u n -> q s n u"))

        def w1_pass(c):
            for fh in range(F // WIDE):
                regroup(w1_mx[c][fh], w1_raw[c][:, :, WIDE * fh : WIDE * fh + WIDE], W1_VECTOR_COLS)
            for fh in range(F // WIDE):
                quantise(w1_mx[c][fh])

        h_ps = {}

        def mm1_pass(ft, half, c):
            if c == 0:
                h_ps[(ft, half)] = psum_h.tile([P, WIDE], F32, name="h_ps", tag="h")
            fh, part = divmod(ft, PARTS)
            mx_pass(h_ps[(ft, half)], w1_mx[c][fh], part, x_mx[c][half], c)

        def relu(ft, half):
            c, t = divmod(ft, PACK)
            nc.scalar.activation(
                out=h_t[c][half][:, t, :],
                in_=h_ps[(ft, half)][:],
                func=ACT.Relu,
                bias=b1_col[:, ft : ft + 1],
                scale=1.0,
            )

        def h_pass(c, half):
            regroup(h_mx[c][half], h_t[c][half][:], WIDE)
            quantise(h_mx[c][half])

        def w2_passes():
            for c in range(PASSES):
                regroup(w2_mx[c], w2_raw[c][:], WIDE)
            for c in range(PASSES):
                quantise(w2_mx[c])

        def v_pair(i):
            for s in range(2):
                j = 2 * i + s
                half, part = divmod(j, PARTS)
                if half == 0:
                    v_ps = psum_v.tile([P, M], F32, name="v_ps", tag="v")
                else:
                    v_ps = psum_h.tile([P, M], F32, name="v_ps_late", tag="h")
                for c in range(PASSES):
                    mx_pass(v_ps, h_mx[c][half], part, w2_mx[c], c)
                nc.vector.tensor_tensor(out=v_sb[j][:], in0=v_ps[:], in1=b2_all[:], op=ALU.add)
                nc.scalar.activation(out=squares[:], in_=v_sb[j][:], func=ACT.Square, accum_out=sumsq[i][:, s : s + 1])

        def normalise_pair(i):
            nc.vector.tensor_scalar_max(out=floored[i][:], in0=sumsq[i][:], scalar1=EPS * EPS)
            nc.scalar.activation(out=norm[i][:], in_=floored[i][:], func=ACT.Sqrt)
            nc.vector.reciprocal(out=inv_norm[i][:], in_=norm[i][:])
            for s in range(2):
                j = 2 * i + s
                nc.vector.tensor_scalar_mul(out=out_sb[j][:], in0=v_sb[j][:], scalar1=inv_norm[i][:, s : s + 1])
                nc.sync.dma_start(out=out_view[:, j, :], in_=out_sb[j][:])

        x_pair(0)
        w1_pass(0)
        x_pair(1)
        for c in range(PASSES):
            quantise(x_mx[c][0])
        for ft in range(H_BANKS):
            mm1_pass(ft, 0, 0)
        w1_pass(1)
        biases()
        for ft in range(H_BANKS):
            mm1_pass(ft, 0, 1)
            relu(ft, 0)
        x_pair(2)
        x_pair(3)
        for c in range(PASSES):
            quantise(x_mx[c][1])
        for ft in range(H_BANKS, FEATURE_TILES):
            for c in range(PASSES):
                mm1_pass(ft, 0, c)
            relu(ft, 0)
        for c in range(PASSES):
            h_pass(c, 0)
        w2_passes()
        for ft in range(FEATURE_TILES):
            for c in range(PASSES):
                mm1_pass(ft, 1, c)
            relu(ft, 1)
            if ft % PACK == PACK - 1:
                h_pass(ft // PACK, 1)
        for i in range(2):
            v_pair(i)
            normalise_pair(i)
        v_pair(2)
        v_pair(3)
        normalise_pair(2)
        normalise_pair(3)
